import numpy as np
import ml_dtypes


def mxq(x, axis, fmt="e4m3"):
    dtype, down = {"e4m3": (ml_dtypes.float8_e4m3fn, 7), "e5m2": (ml_dtypes.float8_e5m2, 14)}[fmt]
    v = np.moveaxis(np.asarray(x, np.float32).astype(ml_dtypes.bfloat16).astype(np.float64), axis, -1)
    blocks = v.reshape(v.shape[:-1] + (-1, 32))
    amax = np.abs(blocks).max(-1, keepdims=True)
    byte = np.maximum(np.where(amax > 0, np.frexp(amax)[1] - 1 + 127, 0) - down, 1)
    scale = np.exp2(byte - 127.0)
    codes = (blocks / scale).astype(np.float32).astype(dtype).astype(np.float64)
    return np.moveaxis((codes * scale).reshape(v.shape), -1, axis)


WIDE = False


def mx_kscale(k):
    if not WIDE:
        return np.ones(k)
    levels = np.array([10, -10, 5, -5, 0])
    a = np.random.permutation(np.resize(levels, k // 512 * 4)).reshape(k // 512, 4)
    idx = np.arange(k)
    return np.exp2(a[idx // 512, idx % 128 // 32])


BF16 = ml_dtypes.bfloat16


def bf(x):
    return np.asarray(x, np.float32).astype(BF16)


def f64(x):
    return np.asarray(x).astype(np.float64)


B, S, D, H, NS = 2, 512, 1024, 8, 3
DH = D // H


def heads(x):
    return x.reshape(B, S, H, DH).transpose(0, 2, 1, 3)


def setup_inputs():
    s = mx_kscale(D)

    def stream():
        return bf(np.random.standard_normal((B, S, D)) * s)

    def weight():
        return bf(np.random.standard_normal((D, D)) / np.sqrt(D) / s[:, None])

    def bias():
        return bf(np.random.standard_normal(D) * 0.1)

    w = (0.4 + 0.3 * np.random.random((NS, NS))) * np.sign(np.random.standard_normal((NS, NS)))
    return {"input_tensor": stream(), "position_embedding": stream(), "attr": stream(),
            "Wq": weight(), "bq": bias(), "Wqp": weight(), "bqp": bias(), "Wqa": weight(), "bqa": bias(),
            "w_matrix": bf(w)}


def reference(input_tensor, position_embedding, attr, Wq, bq, Wqp, bqp, Wqa, bqa, w_matrix):
    Qi = heads((mxq(f64(input_tensor), 2, "e4m3") @ mxq(f64(Wq), 0, "e4m3")) + f64(bq))
    Qp = heads((mxq(f64(position_embedding), 2, "e4m3") @ mxq(f64(Wqp), 0, "e4m3")) + f64(bqp))
    Qa = heads((mxq(f64(attr), 2, "e4m3") @ mxq(f64(Wqa), 0, "e4m3")) + f64(bqa))
    w = f64(w_matrix)
    Q_ki = w[0, 0] * Qi + w[1, 0] * Qp + w[2, 0] * Qa
    Q_kp = w[0, 1] * Qi + w[1, 1] * Qp + w[2, 1] * Qa
    Q_ka = w[0, 2] * Qi + w[1, 2] * Qp + w[2, 2] * Qa
    return Q_ki, Q_kp, Q_ka

@@ -1,0 +1,258 @@
+from contextlib import ExitStack
+
+import concourse.masks as masks
+import concourse.mybir as mybir
+
+F32 = mybir.dt.float32
+BF16 = mybir.dt.bfloat16
+U32 = mybir.dt.uint32
+U8 = mybir.dt.uint8
+FP8X4 = mybir.dt.float8_e4m3fn_x4
+MULT = mybir.AluOpType.mult
+ADD = mybir.AluOpType.add
+COPY = mybir.ActivationFunctionType.Copy
+
+P = 128
+PACK = 4
+K_PASS = P * PACK
+BATCH, SEQ, D, HEADS, NS = 2, 512, 1024, 8, 3
+DH = D // HEADS
+PASSES = D // K_PASS
+HALF = 512
+HALVES = D // HALF
+HEADS_PER_HALF = HALF // DH
+TILES_PER_BATCH = SEQ // P
+TOKEN_TILES = BATCH * TILES_PER_BATCH
+ROUNDS = HALVES * TOKEN_TILES
+ROUNDS_PER_STORE = 2
+RUN = 4
+VECTOR_COLUMNS = 384
+
+FLOPS = 2 * NS * BATCH * SEQ * D * D
+
+
+def tile_crossmultiheadattention_pa_kernel(
+    tc, input_tensor, position_embedding, attr, Wq, bq, Wqp, bqp, Wqa, bqa, w_matrix,
+    out_0, out_1, out_2,
+):
+    nc = tc.nc
+    streams = [input_tensor, position_embedding, attr]
+    weights = [Wq, Wqp, Wqa]
+    biases = [bq, bqp, bqa]
+    outs = [out_0, out_1, out_2]
+    pieces = [(i, g) for i in range(NS) for g in range(PASSES)]
+
+    with ExitStack() as ctx:
+        keep = ctx.enter_context(tc.tile_pool(name="keep", bufs=1))
+        w_raw_pool = ctx.enter_context(tc.tile_pool(name="w_raw", bufs=len(pieces)))
+        w_grouped_pool = ctx.enter_context(tc.tile_pool(name="w_grouped", bufs=3))
+        x_grouped_pool = ctx.enter_context(tc.tile_pool(name="x_grouped", bufs=2))
+        item_pool = ctx.enter_context(tc.tile_pool(name="item", bufs=3))
+        mixed_pool = ctx.enter_context(tc.tile_pool(name="mixed", bufs=3))
+        q_psum = ctx.enter_context(tc.psum_pool(name="q_psum", bufs=2))
+        t_psum = ctx.enter_context(tc.psum_pool(name="t_psum", bufs=2))
+
+        x_codes = keep.tile([P, NS, TOKEN_TILES, PASSES * P], U32, align_bytes=64)
+        x_scales = keep.tile([P, NS, TOKEN_TILES, PASSES * P], U8, align_bytes=64)
+        w_codes = keep.tile([P, NS, PASSES, D], U32, align_bytes=64)
+        w_scales = keep.tile([P, NS, PASSES, D], U8, align_bytes=64)
+
+        x_raw = {}
+        x_grouped = {}
+        w_raw = {}
+        w_grouped = {}
+        q_banks = {}
+        mixed = {}
+
+        def load_x(tau):
+            batch, m = divmod(tau, TILES_PER_BATCH)
+            for i in range(NS):
+                x_raw[i, tau] = keep.tile([P, D], BF16, name="x_raw_%d_%d" % (i, tau))
+                rows = streams[i][batch].rearrange("(p m) k -> p m k", m=TILES_PER_BATCH)
+                nc.sync.dma_start(out=x_raw[i, tau][:], in_=rows[:, m, :])
+
+        def load_w(i, g, half):
+            raw = w_raw_pool.tile([P, PACK, HALF], BF16)
+            rows = weights[i][g * K_PASS : (g + 1) * K_PASS, half * HALF : (half + 1) * HALF]
+            nc.sync.dma_start(out=raw[:], in_=rows.rearrange("(p t) n -> p t n", t=PACK))
+            w_raw[i, g, half] = raw
+
+        def regroup_w(copy, i, g, half, first, last):
+            copy(
+                out=w_grouped[i, g, half][:, first:last, :].rearrange(
+                    "p (c r) t -> p c t r", r=RUN
+                ),
+                in_=w_raw[i, g, half][:, :, first:last].rearrange("p t (c r) -> p c t r", r=RUN),
+            )
+
+        def new_w_grouped(i, g, half):
+            grouped = w_grouped_pool.tile([P, HALF, PACK], BF16, align_bytes=64)
+            w_grouped[i, g, half] = grouped
+
+        def quantise_w(i, g, half):
+            cols = slice(half * HALF, (half + 1) * HALF)
+            nc.vector.quantize_mx(
+                out=w_codes[:, i, g, cols].bitcast(FP8X4),
+                scales=w_scales[:, i, g, cols],
+                in_=w_grouped[i, g, half][:].rearrange("p n t -> p (n t)"),
+            )
+
+        def transpose_x(tau):
+            grouped = x_grouped_pool.tile([P, NS, D], BF16, align_bytes=64)
+            x_grouped[tau] = grouped
+            for i in range(NS):
+                words = x_raw[i, tau][:].bitcast(F32).rearrange(
+                    "r (g p u) -> r g u p", g=PASSES, u=2
+                )
+                turned = t_psum.tile([P, PASSES * 2, P], F32, tag="t_bank")
+                for g in range(PASSES):
+                    for u in range(2):
+                        nc.tensor.transpose(turned[:, 2 * g + u, :], words[:, g, u, :], ident[:])
+                nc.scalar.copy(
+                    out=grouped[:, i, :].bitcast(F32).rearrange(
+                        "p (g r u) -> p g r u", g=PASSES, u=2
+                    ),
+                    in_=turned[:].rearrange("p (g u) r -> p g r u", u=2),
+                )
+
+        def quantise_x(i, tau):
+            nc.vector.quantize_mx(
+                out=x_codes[:, i, tau, :].bitcast(FP8X4),
+                scales=x_scales[:, i, tau, :],
+                in_=x_grouped[tau][:, i, :],
+            )
+
+        def project(i, r):
+            half, tau = divmod(r, TOKEN_TILES)
+            cols = slice(half * HALF, (half + 1) * HALF)
+            bank = q_psum.tile([P, HALF], F32, name="q_%d" % i, tag="q_%d" % i)
+            q_banks[i, r] = bank
+            for g in range(PASSES):
+                tokens = slice(g * P, (g + 1) * P)
+                nc.tensor.matmul_mx(
+                    out=bank[:],
+                    lhsT=x_codes[:, i, tau, tokens].bitcast(FP8X4),
+                    lhsT_scale=x_scales[:, i, tau, tokens],
+                    rhs=w_codes[:, i, g, cols].bitcast(FP8X4),
+                    rhs_scale=w_scales[:, i, g, cols],
+                    start=(g == 0),
+                    stop=(g == PASSES - 1),
+                )
+
+        def by_head(ap):
+            return ap.rearrange("p (h c) -> p h c", c=DH)
+
+        def mix(r):
+            half, tau = divmod(r, TOKEN_TILES)
+            batch, m = divmod(tau, TILES_PER_BATCH)
+            store, place = divmod(m, ROUNDS_PER_STORE)
+            cols = slice(half * HALF, (half + 1) * HALF)
+            if place == 0:
+                for j in range(NS):
+                    mixed[j] = mixed_pool.tile(
+                        [P, HEADS_PER_HALF, ROUNDS_PER_STORE, DH], F32,
+                        name="mixed_%d" % j, tag="mixed_%d" % j,
+                    )
+            item = item_pool.tile([P, NS, HALF], F32)
+            for j in range(NS):
+                nc.scalar.activation(
+                    out=item[:, j, :], in_=q_banks[0, r][:], func=COPY,
+                    scale=w_scalar[:, j : j + 1],
+                )
+            for j in range(NS):
+                nc.vector.scalar_tensor_tensor(
+                    out=mixed[j][:, :, place, :], in0=by_head(q_banks[1, r][:]),
+                    scalar=w_scalar[:, NS + j : NS + j + 1], in1=by_head(bias_mix[:, j, cols]),
+                    op0=MULT, op1=ADD,
+                )
+            for j in range(NS):
+                nc.vector.scalar_tensor_tensor(
+                    out=mixed[j][:, :, place, :], in0=by_head(q_banks[2, r][:]),
+                    scalar=w_scalar[:, 2 * NS + j : 2 * NS + j + 1],
+                    in1=mixed[j][:, :, place, :], op0=MULT, op1=ADD,
+                )
+            for j in range(NS):
+                nc.gpsimd.tensor_tensor(
+                    out=mixed[j][:, :, place, :], in0=mixed[j][:, :, place, :],
+                    in1=by_head(item[:, j, :]), op=ADD,
+                )
+            if place == ROUNDS_PER_STORE - 1:
+                heads = slice(half * HEADS_PER_HALF, (half + 1) * HEADS_PER_HALF)
+                tiles = slice(store * ROUNDS_PER_STORE, (store + 1) * ROUNDS_PER_STORE)
+                for j in range(NS):
+                    rows = outs[j][batch, heads].rearrange(
+                        "h (p m) c -> p h m c", m=TILES_PER_BATCH
+                    )
+                    nc.sync.dma_start(out=rows[:, :, tiles, :], in_=mixed[j][:])
+
+        ident = keep.tile([P, P], F32)
+        masks.make_identity(nc, ident[:])
+        w_rows = keep.tile([P, NS], BF16)
+        bias_rows = keep.tile([P, D], BF16)
+        nc.vector.memset(w_rows[:], 0.0)
+        nc.vector.memset(bias_rows[:], 0.0)
+        nc.scalar.dma_start(out=w_rows[0:NS, :], in_=w_matrix)
+        for i in range(NS):
+            nc.scalar.dma_start(
+                out=bias_rows[i : i + 1, :], in_=biases[i].rearrange("(o n) -> o n", o=1)
+            )
+        w_bf16 = keep.tile([P, NS * NS], BF16)
+        w_scalar = keep.tile([P, NS * NS], F32)
+        nc.scalar.dma_start(
+            out=w_bf16[:], in_=w_matrix.rearrange("i j -> (i j)").partition_broadcast(P)
+        )
+
+        load_x(0)
+        for i, g in pieces:
+            load_w(i, g, 0)
+        load_x(1)
+
+        nc.vector.tensor_copy(out=w_scalar[:], in_=w_bf16[:])
+
+        bias_mix = keep.tile([P, NS, D], F32)
+        for j in range(NS):
+            for half in range(HALVES):
+                cols = slice(half * HALF, (half + 1) * HALF)
+                spread = t_psum.tile([P, HALF], F32, tag="t_bank")
+                nc.tensor.matmul(
+                    out=spread[:], lhsT=w_rows[:, j : j + 1].to_broadcast([P, P]),
+                    rhs=bias_rows[:, cols], start=True, stop=True,
+                )
+                if half == 0:
+                    nc.scalar.copy(out=bias_mix[:, j, cols], in_=spread[:])
+                else:
+                    nc.vector.tensor_copy(out=bias_mix[:, j, cols], in_=spread[:])
+
+        transpose_x(0)
+        for i in range(NS):
+            for g in range(PASSES):
+                new_w_grouped(i, g, 0)
+                regroup_w(nc.vector.tensor_copy, i, g, 0, 0, VECTOR_COLUMNS)
+                regroup_w(nc.scalar.copy, i, g, 0, VECTOR_COLUMNS, HALF)
+            quantise_x(i, 0)
+            for g in range(PASSES):
+                quantise_w(i, g, 0)
+            project(i, 0)
+        transpose_x(1)
+        for i in range(NS):
+            quantise_x(i, 1)
+
+        for tau in range(2, TOKEN_TILES):
+            load_x(tau)
+            load_w(pieces[tau - 2][0], pieces[tau - 2][1], 1)
+
+        for r in range(ROUNDS):
+            if r + 1 < ROUNDS:
+                for i in range(NS):
+                    project(i, r + 1)
+            mix(r)
+            if r + 2 < TOKEN_TILES:
+                transpose_x(r + 2)
+            if r < len(pieces):
+                new_w_grouped(pieces[r][0], pieces[r][1], 1)
+                regroup_w(nc.scalar.copy, pieces[r][0], pieces[r][1], 1, 0, HALF)
+            if r + 2 < TOKEN_TILES:
+                for i in range(NS):
+                    quantise_x(i, r + 2)
+            if 1 <= r <= len(pieces):
+                quantise_w(pieces[r - 1][0], pieces[r - 1][1], 1)

@@ -25,6 +25,7 @@ TILES_PER_BATCH = SEQ // P
 TOKEN_TILES = BATCH * TILES_PER_BATCH
 ROUNDS = HALVES * TOKEN_TILES
 ROUNDS_PER_STORE = 2
+ITEM_LEAD = 2
 RUN = 4
 VECTOR_COLUMNS = 384
 
@@ -142,14 +143,14 @@ def tile_crossmultiheadattention_pa_kernel(
         def by_head(ap):
             return ap.rearrange("p (h c) -> p h c", c=DH)
 
-        def mix(r):
-            half, tau = divmod(r, TOKEN_TILES)
-            batch, m = divmod(tau, TILES_PER_BATCH)
-            store, place = divmod(m, ROUNDS_PER_STORE)
+        def begin_mix(r):
+            half = r // TOKEN_TILES
+            store, place = divmod(r, ROUNDS_PER_STORE)
             cols = slice(half * HALF, (half + 1) * HALF)
+            project(0, r)
             if place == 0:
                 for j in range(NS):
-                    mixed[j] = mixed_pool.tile(
+                    mixed[j, store] = mixed_pool.tile(
                         [P, HEADS_PER_HALF, ROUNDS_PER_STORE, DH], F32,
                         name="mixed_%d" % j, tag="mixed_%d" % j,
                     )
@@ -160,30 +161,30 @@ def tile_crossmultiheadattention_pa_kernel(
                     scale=w_scalar[:, j : j + 1],
                 )
             for j in range(NS):
-                nc.vector.scalar_tensor_tensor(
-                    out=mixed[j][:, :, place, :], in0=by_head(q_banks[1, r][:]),
-                    scalar=w_scalar[:, NS + j : NS + j + 1], in1=by_head(bias_mix[:, j, cols]),
-                    op0=MULT, op1=ADD,
-                )
-            for j in range(NS):
-                nc.vector.scalar_tensor_tensor(
-                    out=mixed[j][:, :, place, :], in0=by_head(q_banks[2, r][:]),
-                    scalar=w_scalar[:, 2 * NS + j : 2 * NS + j + 1],
-                    in1=mixed[j][:, :, place, :], op0=MULT, op1=ADD,
-                )
-            for j in range(NS):
                 nc.gpsimd.tensor_tensor(
-                    out=mixed[j][:, :, place, :], in0=mixed[j][:, :, place, :],
-                    in1=by_head(item[:, j, :]), op=ADD,
+                    out=mixed[j, store][:, :, place, :], in0=by_head(item[:, j, :]),
+                    in1=by_head(bias_mix[:, j, cols]), op=ADD,
                 )
+
+        def finish_mix(r):
+            half, tau = divmod(r, TOKEN_TILES)
+            batch, m = divmod(tau, TILES_PER_BATCH)
+            store, place = divmod(r, ROUNDS_PER_STORE)
+            for i in range(1, NS):
+                for j in range(NS):
+                    nc.vector.scalar_tensor_tensor(
+                        out=mixed[j, store][:, :, place, :], in0=by_head(q_banks[i, r][:]),
+                        scalar=w_scalar[:, NS * i + j : NS * i + j + 1],
+                        in1=mixed[j, store][:, :, place, :], op0=MULT, op1=ADD,
+                    )
             if place == ROUNDS_PER_STORE - 1:
                 heads = slice(half * HEADS_PER_HALF, (half + 1) * HEADS_PER_HALF)
-                tiles = slice(store * ROUNDS_PER_STORE, (store + 1) * ROUNDS_PER_STORE)
+                tiles = slice(m + 1 - ROUNDS_PER_STORE, m + 1)
                 for j in range(NS):
                     rows = outs[j][batch, heads].rearrange(
                         "h (p m) c -> p h m c", m=TILES_PER_BATCH
                     )
-                    nc.sync.dma_start(out=rows[:, :, tiles, :], in_=mixed[j][:])
+                    nc.sync.dma_start(out=rows[:, :, tiles, :], in_=mixed[j, store][:])
 
         ident = keep.tile([P, P], F32)
         masks.make_identity(nc, ident[:])
@@ -232,27 +233,37 @@ def tile_crossmultiheadattention_pa_kernel(
             quantise_x(i, 0)
             for g in range(PASSES):
                 quantise_w(i, g, 0)
-            project(i, 0)
-        transpose_x(1)
-        for i in range(NS):
-            quantise_x(i, 1)
+            if i == 0:
+                begin_mix(0)
+            else:
+                project(i, 0)
 
         for tau in range(2, TOKEN_TILES):
             load_x(tau)
             load_w(pieces[tau - 2][0], pieces[tau - 2][1], 1)
 
+        for tau in range(1, 1 + ITEM_LEAD):
+            transpose_x(tau)
+            for i in range(NS):
+                quantise_x(i, tau)
+        for r in range(1, ITEM_LEAD):
+            begin_mix(r)
+
         for r in range(ROUNDS):
+            if r + ITEM_LEAD < ROUNDS:
+                begin_mix(r + ITEM_LEAD)
             if r + 1 < ROUNDS:
-                for i in range(NS):
+                for i in range(1, NS):
                     project(i, r + 1)
-            mix(r)
-            if r + 2 < TOKEN_TILES:
-                transpose_x(r + 2)
+            finish_mix(r)
+            next_tile = r + 1 + ITEM_LEAD
+            if next_tile < TOKEN_TILES:
+                transpose_x(next_tile)
             if r < len(pieces):
                 new_w_grouped(pieces[r][0], pieces[r][1], 1)
                 regroup_w(nc.scalar.copy, pieces[r][0], pieces[r][1], 1, 0, HALF)
-            if r + 2 < TOKEN_TILES:
+            if next_tile < TOKEN_TILES:
                 for i in range(NS):
-                    quantise_x(i, r + 2)
+                    quantise_x(i, next_tile)
             if 1 <= r <= len(pieces):
                 quantise_w(pieces[r - 1][0], pieces[r - 1][1], 1)

@@ -25,7 +25,6 @@ TILES_PER_BATCH = SEQ // P
 TOKEN_TILES = BATCH * TILES_PER_BATCH
 ROUNDS = HALVES * TOKEN_TILES
 ROUNDS_PER_STORE = 2
-ITEM_LEAD = 2
 RUN = 4
 VECTOR_COLUMNS = 384
 
@@ -63,7 +62,7 @@ def tile_crossmultiheadattention_pa_kernel(
         w_raw = {}
         w_grouped = {}
         q_banks = {}
-        mixed = {}
+        gathered = {}
 
         def load_x(tau):
             batch, m = divmod(tau, TILES_PER_BATCH)
@@ -143,17 +142,16 @@ def tile_crossmultiheadattention_pa_kernel(
         def by_head(ap):
             return ap.rearrange("p (h c) -> p h c", c=DH)
 
-        def begin_mix(r):
-            half = r // TOKEN_TILES
-            store, place = divmod(r, ROUNDS_PER_STORE)
+        def mix(r):
+            half, tau = divmod(r, TOKEN_TILES)
+            batch, m = divmod(tau, TILES_PER_BATCH)
+            store, place = divmod(m, ROUNDS_PER_STORE)
             cols = slice(half * HALF, (half + 1) * HALF)
-            project(0, r)
             if place == 0:
-                for j in range(NS):
-                    mixed[j, store] = mixed_pool.tile(
-                        [P, HEADS_PER_HALF, ROUNDS_PER_STORE, DH], F32,
-                        name="mixed_%d" % j, tag="mixed_%d" % j,
-                    )
+                gathered["tile"] = mixed_pool.tile(
+                    [P, NS, HEADS_PER_HALF, ROUNDS_PER_STORE, DH], F32, name="mixed"
+                )
+            mixed = gathered["tile"]
             item = item_pool.tile([P, NS, HALF], F32)
             for j in range(NS):
                 nc.scalar.activation(
@@ -161,30 +159,30 @@ def tile_crossmultiheadattention_pa_kernel(
                     scale=w_scalar[:, j : j + 1],
                 )
             for j in range(NS):
-                nc.gpsimd.tensor_tensor(
-                    out=mixed[j, store][:, :, place, :], in0=by_head(item[:, j, :]),
-                    in1=by_head(bias_mix[:, j, cols]), op=ADD,
+                nc.vector.scalar_tensor_tensor(
+                    out=mixed[:, j, :, place, :], in0=by_head(q_banks[1, r][:]),
+                    scalar=w_scalar[:, NS + j : NS + j + 1], in1=by_head(bias_mix[:, j, cols]),
+                    op0=MULT, op1=ADD,
                 )
-
-        def finish_mix(r):
-            half, tau = divmod(r, TOKEN_TILES)
-            batch, m = divmod(tau, TILES_PER_BATCH)
-            store, place = divmod(r, ROUNDS_PER_STORE)
-            for i in range(1, NS):
-                for j in range(NS):
-                    nc.vector.scalar_tensor_tensor(
-                        out=mixed[j, store][:, :, place, :], in0=by_head(q_banks[i, r][:]),
-                        scalar=w_scalar[:, NS * i + j : NS * i + j + 1],
-                        in1=mixed[j, store][:, :, place, :], op0=MULT, op1=ADD,
-                    )
+            for j in range(NS):
+                nc.vector.scalar_tensor_tensor(
+                    out=mixed[:, j, :, place, :], in0=by_head(q_banks[2, r][:]),
+                    scalar=w_scalar[:, 2 * NS + j : 2 * NS + j + 1],
+                    in1=mixed[:, j, :, place, :], op0=MULT, op1=ADD,
+                )
+            this_round = mixed[:].rearrange("p j h s c -> p (j h) s c")[:, :, place, :]
+            nc.gpsimd.tensor_tensor(
+                out=this_round, in0=this_round,
+                in1=item[:].rearrange("p j (h c) -> p (j h) c", c=DH), op=ADD,
+            )
             if place == ROUNDS_PER_STORE - 1:
                 heads = slice(half * HEADS_PER_HALF, (half + 1) * HEADS_PER_HALF)
-                tiles = slice(m + 1 - ROUNDS_PER_STORE, m + 1)
+                tiles = slice(store * ROUNDS_PER_STORE, (store + 1) * ROUNDS_PER_STORE)
                 for j in range(NS):
                     rows = outs[j][batch, heads].rearrange(
                         "h (p m) c -> p h m c", m=TILES_PER_BATCH
                     )
-                    nc.sync.dma_start(out=rows[:, :, tiles, :], in_=mixed[j, store][:])
+                    nc.sync.dma_start(out=rows[:, :, tiles, :], in_=mixed[:, j])
 
         ident = keep.tile([P, P], F32)
         masks.make_identity(nc, ident[:])
@@ -233,37 +231,27 @@ def tile_crossmultiheadattention_pa_kernel(
             quantise_x(i, 0)
             for g in range(PASSES):
                 quantise_w(i, g, 0)
-            if i == 0:
-                begin_mix(0)
-            else:
-                project(i, 0)
+            project(i, 0)
+        transpose_x(1)
+        for i in range(NS):
+            quantise_x(i, 1)
 
         for tau in range(2, TOKEN_TILES):
             load_x(tau)
             load_w(pieces[tau - 2][0], pieces[tau - 2][1], 1)
 
-        for tau in range(1, 1 + ITEM_LEAD):
-            transpose_x(tau)
-            for i in range(NS):
-                quantise_x(i, tau)
-        for r in range(1, ITEM_LEAD):
-            begin_mix(r)
-
         for r in range(ROUNDS):
-            if r + ITEM_LEAD < ROUNDS:
-                begin_mix(r + ITEM_LEAD)
             if r + 1 < ROUNDS:
-                for i in range(1, NS):
+                for i in range(NS):
                     project(i, r + 1)
-            finish_mix(r)
-            next_tile = r + 1 + ITEM_LEAD
-            if next_tile < TOKEN_TILES:
-                transpose_x(next_tile)
+            mix(r)
+            if r + 2 < TOKEN_TILES:
+                transpose_x(r + 2)
             if r < len(pieces):
                 new_w_grouped(pieces[r][0], pieces[r][1], 1)
                 regroup_w(nc.scalar.copy, pieces[r][0], pieces[r][1], 1, 0, HALF)
-            if next_tile < TOKEN_TILES:
+            if r + 2 < TOKEN_TILES:
                 for i in range(NS):
-                    quantise_x(i, next_tile)
+                    quantise_x(i, r + 2)
             if 1 <= r <= len(pieces):
                 quantise_w(pieces[r - 1][0], pieces[r - 1][1], 1)

@@ -10,7 +10,7 @@ U8 = mybir.dt.uint8
 FP8X4 = mybir.dt.float8_e4m3fn_x4
 MULT = mybir.AluOpType.mult
 ADD = mybir.AluOpType.add
-COPY = mybir.ActivationFunctionType.Copy
+IDENTITY = mybir.ActivationFunctionType.Identity
 
 P = 128
 PACK = 4
@@ -18,15 +18,15 @@ K_PASS = P * PACK
 BATCH, SEQ, D, HEADS, NS = 2, 512, 1024, 8, 3
 DH = D // HEADS
 PASSES = D // K_PASS
-HALF = 512
-HALVES = D // HALF
-HEADS_PER_HALF = HALF // DH
-TILES_PER_BATCH = SEQ // P
-TOKEN_TILES = BATCH * TILES_PER_BATCH
-ROUNDS = HALVES * TOKEN_TILES
-ROUNDS_PER_STORE = 2
+TILES = SEQ // P
+ROUNDS = BATCH * HEADS
+PIECE = 256
+QUARTERS = D // PIECE
+PIECES_PER_ROUND = 3
 RUN = 4
-VECTOR_COLUMNS = 384
+VECTOR_COLUMNS = 160
+X_TURN_ROUND = 4
+LOAD_AHEAD = 3
 
 FLOPS = 2 * NS * BATCH * SEQ * D * D
 
@@ -40,20 +40,22 @@ def tile_crossmultiheadattention_pa_kernel(
     weights = [Wq, Wqp, Wqa]
     biases = [bq, bqp, bqa]
     outs = [out_0, out_1, out_2]
-    pieces = [(i, g) for i in range(NS) for g in range(PASSES)]
+    later_pieces = [
+        (i, g, q) for q in range(1, QUARTERS) for i in range(NS) for g in range(PASSES)
+    ]
 
     with ExitStack() as ctx:
         keep = ctx.enter_context(tc.tile_pool(name="keep", bufs=1))
-        w_raw_pool = ctx.enter_context(tc.tile_pool(name="w_raw", bufs=len(pieces)))
-        w_grouped_pool = ctx.enter_context(tc.tile_pool(name="w_grouped", bufs=3))
         x_grouped_pool = ctx.enter_context(tc.tile_pool(name="x_grouped", bufs=2))
-        item_pool = ctx.enter_context(tc.tile_pool(name="item", bufs=3))
-        mixed_pool = ctx.enter_context(tc.tile_pool(name="mixed", bufs=3))
-        q_psum = ctx.enter_context(tc.psum_pool(name="q_psum", bufs=2))
-        t_psum = ctx.enter_context(tc.psum_pool(name="t_psum", bufs=2))
+        w_grouped_pool = ctx.enter_context(tc.tile_pool(name="w_grouped", bufs=2 * PIECES_PER_ROUND))
+        mix_pool = ctx.enter_context(tc.tile_pool(name="mix", bufs=3))
+        out_pool = ctx.enter_context(tc.tile_pool(name="out", bufs=3))
+        ahead_psum = ctx.enter_context(tc.psum_pool(name="ahead_psum", bufs=2))
+        single_psum = ctx.enter_context(tc.psum_pool(name="single_psum", bufs=1))
+        turn_psum = ctx.enter_context(tc.psum_pool(name="turn_psum", bufs=4))
 
-        x_codes = keep.tile([P, NS, TOKEN_TILES, PASSES * P], U32, align_bytes=64)
-        x_scales = keep.tile([P, NS, TOKEN_TILES, PASSES * P], U8, align_bytes=64)
+        x_codes = keep.tile([P, NS, BATCH, PASSES * SEQ], U32, align_bytes=64)
+        x_scales = keep.tile([P, NS, BATCH, PASSES * SEQ], U8, align_bytes=64)
         w_codes = keep.tile([P, NS, PASSES, D], U32, align_bytes=64)
         w_scales = keep.tile([P, NS, PASSES, D], U8, align_bytes=64)
 
@@ -61,197 +63,215 @@ def tile_crossmultiheadattention_pa_kernel(
         x_grouped = {}
         w_raw = {}
         w_grouped = {}
-        q_banks = {}
-        gathered = {}
+        banks = {}
+        mixes = {}
+        turned_back = {}
 
-        def load_x(tau):
-            batch, m = divmod(tau, TILES_PER_BATCH)
-            for i in range(NS):
-                x_raw[i, tau] = keep.tile([P, D], BF16, name="x_raw_%d_%d" % (i, tau))
-                rows = streams[i][batch].rearrange("(p m) k -> p m k", m=TILES_PER_BATCH)
-                nc.sync.dma_start(out=x_raw[i, tau][:], in_=rows[:, m, :])
+        def load_x(i, batch):
+            x_raw[i, batch] = keep.tile([P, TILES, D], BF16, name="x_raw_%d_%d" % (i, batch))
+            rows = streams[i][batch].rearrange("(p m) k -> p m k", m=TILES)
+            for m in range(TILES):
+                nc.sync.dma_start(out=x_raw[i, batch][:, m, :], in_=rows[:, m, :])
 
-        def load_w(i, g, half):
-            raw = w_raw_pool.tile([P, PACK, HALF], BF16)
-            rows = weights[i][g * K_PASS : (g + 1) * K_PASS, half * HALF : (half + 1) * HALF]
-            nc.sync.dma_start(out=raw[:], in_=rows.rearrange("(p t) n -> p t n", t=PACK))
-            w_raw[i, g, half] = raw
+        def load_w(piece):
+            i, g, q = piece
+            w_raw[piece] = keep.tile([P, PACK, PIECE], BF16, name="w_raw_%d_%d_%d" % piece)
+            rows = weights[i][g * K_PASS : (g + 1) * K_PASS, q * PIECE : (q + 1) * PIECE]
+            nc.sync.dma_start(out=w_raw[piece][:], in_=rows.rearrange("(p t) n -> p t n", t=PACK))
 
-        def regroup_w(copy, i, g, half, first, last):
+        def pieces_of(r):
+            return later_pieces[r * PIECES_PER_ROUND : (r + 1) * PIECES_PER_ROUND]
+
+        def load_for(r):
+            for piece in pieces_of(r):
+                load_w(piece)
+            if 0 <= r - X_TURN_ROUND < NS:
+                load_x(r - X_TURN_ROUND, 1)
+
+        def regroup_w(copy, piece, first, last):
             copy(
-                out=w_grouped[i, g, half][:, first:last, :].rearrange(
-                    "p (c r) t -> p c t r", r=RUN
-                ),
-                in_=w_raw[i, g, half][:, :, first:last].rearrange("p t (c r) -> p c t r", r=RUN),
+                out=w_grouped[piece][:, first:last, :].rearrange("p (c r) t -> p c t r", r=RUN),
+                in_=w_raw[piece][:, :, first:last].rearrange("p t (c r) -> p c t r", r=RUN),
             )
 
-        def new_w_grouped(i, g, half):
-            grouped = w_grouped_pool.tile([P, HALF, PACK], BF16, align_bytes=64)
-            w_grouped[i, g, half] = grouped
+        def scalar_share(piece):
+            w_grouped[piece] = w_grouped_pool.tile(
+                [P, PIECE, PACK], BF16, name="w_grouped", align_bytes=64
+            )
+            regroup_w(nc.scalar.copy, piece, VECTOR_COLUMNS, PIECE)
 
-        def quantise_w(i, g, half):
-            cols = slice(half * HALF, (half + 1) * HALF)
+        def vector_share(piece):
+            regroup_w(nc.vector.tensor_copy, piece, 0, VECTOR_COLUMNS)
+
+        def quantise_w(piece):
+            i, g, q = piece
+            cols = slice(q * PIECE, (q + 1) * PIECE)
             nc.vector.quantize_mx(
                 out=w_codes[:, i, g, cols].bitcast(FP8X4),
                 scales=w_scales[:, i, g, cols],
-                in_=w_grouped[i, g, half][:].rearrange("p n t -> p (n t)"),
+                in_=w_grouped[piece][:].rearrange("p n t -> p (n t)"),
             )
 
-        def transpose_x(tau):
-            grouped = x_grouped_pool.tile([P, NS, D], BF16, align_bytes=64)
-            x_grouped[tau] = grouped
-            for i in range(NS):
-                words = x_raw[i, tau][:].bitcast(F32).rearrange(
+        def turn_x(i, batch):
+            grouped = x_grouped_pool.tile([P, PASSES, TILES, P * PACK], BF16, align_bytes=64)
+            x_grouped[i, batch] = grouped
+            for m in range(TILES):
+                words = x_raw[i, batch][:].bitcast(F32)[:, m, :].rearrange(
                     "r (g p u) -> r g u p", g=PASSES, u=2
                 )
-                turned = t_psum.tile([P, PASSES * 2, P], F32, tag="t_bank")
+                turned = turn_psum.tile([P, PASSES * 2, P], F32, tag="turn")
                 for g in range(PASSES):
                     for u in range(2):
                         nc.tensor.transpose(turned[:, 2 * g + u, :], words[:, g, u, :], ident[:])
                 nc.scalar.copy(
-                    out=grouped[:, i, :].bitcast(F32).rearrange(
-                        "p (g r u) -> p g r u", g=PASSES, u=2
-                    ),
+                    out=grouped[:].bitcast(F32)[:, :, m, :].rearrange("p g (r u) -> p g r u", u=2),
                     in_=turned[:].rearrange("p (g u) r -> p g r u", u=2),
                 )
 
-        def quantise_x(i, tau):
+        def quantise_x(i, batch):
             nc.vector.quantize_mx(
-                out=x_codes[:, i, tau, :].bitcast(FP8X4),
-                scales=x_scales[:, i, tau, :],
-                in_=x_grouped[tau][:, i, :],
+                out=x_codes[:, i, batch, :].bitcast(FP8X4),
+                scales=x_scales[:, i, batch, :],
+                in_=x_grouped[i, batch][:].rearrange("p g m c -> p (g m c)"),
             )
 
         def project(i, r):
-            half, tau = divmod(r, TOKEN_TILES)
-            cols = slice(half * HALF, (half + 1) * HALF)
-            bank = q_psum.tile([P, HALF], F32, name="q_%d" % i, tag="q_%d" % i)
-            q_banks[i, r] = bank
+            batch, head = divmod(r, HEADS)
+            features = slice(head * DH, (head + 1) * DH)
+            pool = ahead_psum if i == 0 else single_psum
+            bank = pool.tile([P, SEQ], F32, name="p_%d" % i, tag="p_%d" % i)
+            banks[i, r] = bank
             for g in range(PASSES):
-                tokens = slice(g * P, (g + 1) * P)
+                tokens = slice(g * SEQ, (g + 1) * SEQ)
                 nc.tensor.matmul_mx(
                     out=bank[:],
-                    lhsT=x_codes[:, i, tau, tokens].bitcast(FP8X4),
-                    lhsT_scale=x_scales[:, i, tau, tokens],
-                    rhs=w_codes[:, i, g, cols].bitcast(FP8X4),
-                    rhs_scale=w_scales[:, i, g, cols],
+                    lhsT=w_codes[:, i, g, features].bitcast(FP8X4),
+                    lhsT_scale=w_scales[:, i, g, features],
+                    rhs=x_codes[:, i, batch, tokens].bitcast(FP8X4),
+                    rhs_scale=x_scales[:, i, batch, tokens],
                     start=(g == 0),
                     stop=(g == PASSES - 1),
                 )
 
-        def by_head(ap):
-            return ap.rearrange("p (h c) -> p h c", c=DH)
-
-        def mix(r):
-            half, tau = divmod(r, TOKEN_TILES)
-            batch, m = divmod(tau, TILES_PER_BATCH)
-            store, place = divmod(m, ROUNDS_PER_STORE)
-            cols = slice(half * HALF, (half + 1) * HALF)
-            if place == 0:
-                gathered["tile"] = mixed_pool.tile(
-                    [P, NS, HEADS_PER_HALF, ROUNDS_PER_STORE, DH], F32, name="mixed"
-                )
-            mixed = gathered["tile"]
-            item = item_pool.tile([P, NS, HALF], F32)
+        def begin_mix(r):
+            head = r % HEADS
+            mixes[r] = mix_pool.tile([P, NS, SEQ], F32, name="mix")
             for j in range(NS):
                 nc.scalar.activation(
-                    out=item[:, j, :], in_=q_banks[0, r][:], func=COPY,
-                    scale=w_scalar[:, j : j + 1],
+                    out=mixes[r][:, j, :], in_=banks[0, r][:], func=IDENTITY,
+                    scale=w_scalar[:, j : j + 1], bias=bias_mix[:, j, head : head + 1],
                 )
+
+        def add_stream(i, r):
             for j in range(NS):
                 nc.vector.scalar_tensor_tensor(
-                    out=mixed[:, j, :, place, :], in0=by_head(q_banks[1, r][:]),
-                    scalar=w_scalar[:, NS + j : NS + j + 1], in1=by_head(bias_mix[:, j, cols]),
+                    out=mixes[r][:, j, :], in0=banks[i, r][:],
+                    scalar=w_scalar[:, NS * i + j : NS * i + j + 1], in1=mixes[r][:, j, :],
                     op0=MULT, op1=ADD,
                 )
+
+        def turn_back(r):
             for j in range(NS):
-                nc.vector.scalar_tensor_tensor(
-                    out=mixed[:, j, :, place, :], in0=by_head(q_banks[2, r][:]),
-                    scalar=w_scalar[:, 2 * NS + j : 2 * NS + j + 1],
-                    in1=mixed[:, j, :, place, :], op0=MULT, op1=ADD,
-                )
-            this_round = mixed[:].rearrange("p j h s c -> p (j h) s c")[:, :, place, :]
-            nc.gpsimd.tensor_tensor(
-                out=this_round, in0=this_round,
-                in1=item[:].rearrange("p j (h c) -> p (j h) c", c=DH), op=ADD,
-            )
-            if place == ROUNDS_PER_STORE - 1:
-                heads = slice(half * HEADS_PER_HALF, (half + 1) * HEADS_PER_HALF)
-                tiles = slice(store * ROUNDS_PER_STORE, (store + 1) * ROUNDS_PER_STORE)
-                for j in range(NS):
-                    rows = outs[j][batch, heads].rearrange(
-                        "h (p m) c -> p h m c", m=TILES_PER_BATCH
+                turned_back[j, r] = turn_psum.tile([P, TILES, DH], F32, name="back", tag="turn")
+                for m in range(TILES):
+                    nc.tensor.transpose(
+                        turned_back[j, r][:, m, :], mixes[r][:, j, m * P : (m + 1) * P], ident[:]
                     )
-                    nc.sync.dma_start(out=rows[:, :, tiles, :], in_=mixed[:, j])
+
+        def store(r):
+            batch, head = divmod(r, HEADS)
+            result = out_pool.tile([P, NS, SEQ], F32)
+            for j in range(NS):
+                nc.scalar.copy(
+                    out=result[:, j, :], in_=turned_back[j, r][:].rearrange("p m c -> p (m c)")
+                )
+                nc.sync.dma_start(
+                    out=outs[j][batch, head].rearrange("(p m) c -> p (m c)", m=TILES),
+                    in_=result[:, j, :],
+                )
 
         ident = keep.tile([P, P], F32)
         masks.make_identity(nc, ident[:])
-        w_rows = keep.tile([P, NS], BF16)
-        bias_rows = keep.tile([P, D], BF16)
-        nc.vector.memset(w_rows[:], 0.0)
-        nc.vector.memset(bias_rows[:], 0.0)
-        nc.scalar.dma_start(out=w_rows[0:NS, :], in_=w_matrix)
-        for i in range(NS):
-            nc.scalar.dma_start(
-                out=bias_rows[i : i + 1, :], in_=biases[i].rearrange("(o n) -> o n", o=1)
-            )
         w_bf16 = keep.tile([P, NS * NS], BF16)
         w_scalar = keep.tile([P, NS * NS], F32)
         nc.scalar.dma_start(
             out=w_bf16[:], in_=w_matrix.rearrange("i j -> (i j)").partition_broadcast(P)
         )
+        bias_rows = keep.tile([P, P], BF16)
+        nc.vector.memset(bias_rows[:], 0.0)
+        for i in range(NS):
+            nc.scalar.dma_start(
+                out=bias_rows[i * HEADS : (i + 1) * HEADS, :],
+                in_=biases[i].rearrange("(h c) -> h c", c=DH),
+            )
 
-        load_x(0)
-        for i, g in pieces:
-            load_w(i, g, 0)
-        load_x(1)
+        for i in range(NS):
+            load_x(i, 0)
+            for g in range(PASSES):
+                load_w((i, g, 0))
+        for r in range(LOAD_AHEAD):
+            load_for(r)
 
         nc.vector.tensor_copy(out=w_scalar[:], in_=w_bf16[:])
-
-        bias_mix = keep.tile([P, NS, D], F32)
+        bias_f32 = keep.tile([P, P], F32)
+        nc.vector.tensor_copy(out=bias_f32[:], in_=bias_rows[:])
+        bias_cols = turn_psum.tile([P, P], F32, tag="turn")
+        nc.tensor.transpose(bias_cols[:], bias_f32[:], ident[:])
+        bias_mix = keep.tile([P, NS, HEADS], F32)
         for j in range(NS):
-            for half in range(HALVES):
-                cols = slice(half * HALF, (half + 1) * HALF)
-                spread = t_psum.tile([P, HALF], F32, tag="t_bank")
-                nc.tensor.matmul(
-                    out=spread[:], lhsT=w_rows[:, j : j + 1].to_broadcast([P, P]),
-                    rhs=bias_rows[:, cols], start=True, stop=True,
+            nc.vector.tensor_scalar_mul(
+                out=bias_mix[:, j, :], in0=bias_cols[:, 0:HEADS], scalar1=w_scalar[:, j : j + 1]
+            )
+        for i in range(1, NS):
+            for j in range(NS):
+                nc.vector.scalar_tensor_tensor(
+                    out=bias_mix[:, j, :], in0=bias_cols[:, i * HEADS : (i + 1) * HEADS],
+                    scalar=w_scalar[:, NS * i + j : NS * i + j + 1], in1=bias_mix[:, j, :],
+                    op0=MULT, op1=ADD,
                 )
-                if half == 0:
-                    nc.scalar.copy(out=bias_mix[:, j, cols], in_=spread[:])
-                else:
-                    nc.vector.tensor_copy(out=bias_mix[:, j, cols], in_=spread[:])
 
-        transpose_x(0)
+        ctx.enter_context(tc.manual_schedule())
+
+        turn_x(0, 0)
         for i in range(NS):
             for g in range(PASSES):
-                new_w_grouped(i, g, 0)
-                regroup_w(nc.vector.tensor_copy, i, g, 0, 0, VECTOR_COLUMNS)
-                regroup_w(nc.scalar.copy, i, g, 0, VECTOR_COLUMNS, HALF)
+                scalar_share((i, g, 0))
+                vector_share((i, g, 0))
+            if i + 1 < NS:
+                turn_x(i + 1, 0)
             quantise_x(i, 0)
             for g in range(PASSES):
-                quantise_w(i, g, 0)
+                quantise_w((i, g, 0))
             project(i, 0)
-        transpose_x(1)
-        for i in range(NS):
-            quantise_x(i, 1)
-
-        for tau in range(2, TOKEN_TILES):
-            load_x(tau)
-            load_w(pieces[tau - 2][0], pieces[tau - 2][1], 1)
+        begin_mix(0)
+        project(0, 1)
 
         for r in range(ROUNDS):
+            pieces = pieces_of(r)
+            load_for(r + LOAD_AHEAD)
+            if r >= 1:
+                turn_back(r - 1)
+            for piece in pieces:
+                scalar_share(piece)
             if r + 1 < ROUNDS:
-                for i in range(NS):
-                    project(i, r + 1)
-            mix(r)
-            if r + 2 < TOKEN_TILES:
-                transpose_x(r + 2)
-            if r < len(pieces):
-                new_w_grouped(pieces[r][0], pieces[r][1], 1)
-                regroup_w(nc.scalar.copy, pieces[r][0], pieces[r][1], 1, 0, HALF)
-            if r + 2 < TOKEN_TILES:
-                for i in range(NS):
-                    quantise_x(i, r + 2)
-            if 1 <= r <= len(pieces):
-                quantise_w(pieces[r - 1][0], pieces[r - 1][1], 1)
+                begin_mix(r + 1)
+            if r >= 1:
+                store(r - 1)
+            add_stream(1, r)
+            for piece in pieces:
+                vector_share(piece)
+            if 0 <= r - X_TURN_ROUND - 1 < NS:
+                quantise_x(r - X_TURN_ROUND - 1, 1)
+            for piece in pieces:
+                quantise_w(piece)
+            if 0 <= r - X_TURN_ROUND < NS:
+                turn_x(r - X_TURN_ROUND, 1)
+            add_stream(2, r)
+            if r + 1 < ROUNDS:
+                project(1, r + 1)
+            if r + 2 < ROUNDS:
+                project(0, r + 2)
+            if r + 1 < ROUNDS:
+                project(2, r + 1)
+        turn_back(ROUNDS - 1)
+        store(ROUNDS - 1)

@@ -19,14 +19,18 @@ BATCH, SEQ, D, HEADS, NS = 2, 512, 1024, 8, 3
 DH = D // HEADS
 PASSES = D // K_PASS
 TILES = SEQ // P
-ROUNDS = BATCH * HEADS
 PIECE = 256
-QUARTERS = D // PIECE
-PIECES_PER_ROUND = 3
 RUN = 4
 VECTOR_COLUMNS = 160
-X_TURN_ROUND = 4
-LOAD_AHEAD = 3
+ORDER = [(b, h) for first, last in ((0, 4), (4, 6), (6, 8)) for b in range(BATCH) for h in range(first, last)]
+ROUNDS = len(ORDER)
+W_ROUND = {(0, 1): -1, (1, 1): 0, (2, 1): 1, (0, 2): 4, (1, 2): 5, (2, 2): 6, (0, 3): 8, (1, 3): 9, (2, 3): 10}
+X_ROUND = {0: 1, 1: 2, 2: 3}
+
+
+def scalar_outputs(r):
+    return range(NS - (0 if r < 4 else 1 if r < 11 else 2), NS)
+
 
 FLOPS = 2 * NS * BATCH * SEQ * D * D
 
@@ -40,19 +44,19 @@ def tile_crossmultiheadattention_pa_kernel(
     weights = [Wq, Wqp, Wqa]
     biases = [bq, bqp, bqa]
     outs = [out_0, out_1, out_2]
-    later_pieces = [
-        (i, g, q) for q in range(1, QUARTERS) for i in range(NS) for g in range(PASSES)
-    ]
 
     with ExitStack() as ctx:
         keep = ctx.enter_context(tc.tile_pool(name="keep", bufs=1))
+        x_raw_pool = ctx.enter_context(tc.tile_pool(name="x_raw", bufs=4))
         x_grouped_pool = ctx.enter_context(tc.tile_pool(name="x_grouped", bufs=2))
-        w_grouped_pool = ctx.enter_context(tc.tile_pool(name="w_grouped", bufs=2 * PIECES_PER_ROUND))
-        mix_pool = ctx.enter_context(tc.tile_pool(name="mix", bufs=3))
-        out_pool = ctx.enter_context(tc.tile_pool(name="out", bufs=3))
-        ahead_psum = ctx.enter_context(tc.psum_pool(name="ahead_psum", bufs=2))
-        single_psum = ctx.enter_context(tc.psum_pool(name="single_psum", bufs=1))
-        turn_psum = ctx.enter_context(tc.psum_pool(name="turn_psum", bufs=4))
+        w_grouped_pool = ctx.enter_context(tc.tile_pool(name="w_grouped", bufs=6))
+        mix_pool = ctx.enter_context(tc.tile_pool(name="mix", bufs=4))
+        term_pool = ctx.enter_context(tc.tile_pool(name="term", bufs=3))
+        copied_pool = ctx.enter_context(tc.tile_pool(name="copied", bufs=3))
+        out_pool = ctx.enter_context(tc.tile_pool(name="out", bufs=4))
+        product_psum = ctx.enter_context(tc.psum_pool(name="product_psum", bufs=1))
+        back_psum = ctx.enter_context(tc.psum_pool(name="back_psum", bufs=3))
+        turn_psum = ctx.enter_context(tc.psum_pool(name="turn_psum", bufs=2))
 
         x_codes = keep.tile([P, NS, BATCH, PASSES * SEQ], U32, align_bytes=64)
         x_scales = keep.tile([P, NS, BATCH, PASSES * SEQ], U8, align_bytes=64)
@@ -65,28 +69,22 @@ def tile_crossmultiheadattention_pa_kernel(
         w_grouped = {}
         banks = {}
         mixes = {}
+        terms = {}
+        copied = {}
         turned_back = {}
 
         def load_x(i, batch):
-            x_raw[i, batch] = keep.tile([P, TILES, D], BF16, name="x_raw_%d_%d" % (i, batch))
+            x_raw[i, batch] = x_raw_pool.tile([P, TILES, D], BF16, name="x_raw")
             rows = streams[i][batch].rearrange("(p m) k -> p m k", m=TILES)
             for m in range(TILES):
                 nc.sync.dma_start(out=x_raw[i, batch][:, m, :], in_=rows[:, m, :])
 
-        def load_w(piece):
-            i, g, q = piece
-            w_raw[piece] = keep.tile([P, PACK, PIECE], BF16, name="w_raw_%d_%d_%d" % piece)
-            rows = weights[i][g * K_PASS : (g + 1) * K_PASS, q * PIECE : (q + 1) * PIECE]
-            nc.sync.dma_start(out=w_raw[piece][:], in_=rows.rearrange("(p t) n -> p t n", t=PACK))
-
-        def pieces_of(r):
-            return later_pieces[r * PIECES_PER_ROUND : (r + 1) * PIECES_PER_ROUND]
-
-        def load_for(r):
-            for piece in pieces_of(r):
-                load_w(piece)
-            if 0 <= r - X_TURN_ROUND < NS:
-                load_x(r - X_TURN_ROUND, 1)
+        def load_w(i, q):
+            for g in range(PASSES):
+                tile = keep.tile([P, PACK, PIECE], BF16, name="w_raw_%d_%d_%d" % (i, g, q))
+                w_raw[i, g, q] = tile
+                rows = weights[i][g * K_PASS : (g + 1) * K_PASS, q * PIECE : (q + 1) * PIECE]
+                nc.sync.dma_start(out=tile[:], in_=rows.rearrange("(p t) n -> p t n", t=PACK))
 
         def regroup_w(copy, piece, first, last):
             copy(
@@ -94,32 +92,38 @@ def tile_crossmultiheadattention_pa_kernel(
                 in_=w_raw[piece][:, :, first:last].rearrange("p t (c r) -> p c t r", r=RUN),
             )
 
-        def scalar_share(piece):
-            w_grouped[piece] = w_grouped_pool.tile(
-                [P, PIECE, PACK], BF16, name="w_grouped", align_bytes=64
-            )
-            regroup_w(nc.scalar.copy, piece, VECTOR_COLUMNS, PIECE)
+        def group_w(i, q):
+            for g in range(PASSES):
+                piece = (i, g, q)
+                w_grouped[piece] = w_grouped_pool.tile(
+                    [P, PIECE, PACK], BF16, name="w_grouped", align_bytes=64
+                )
+                if q == 0:
+                    regroup_w(nc.scalar.copy, piece, VECTOR_COLUMNS, PIECE)
+                    regroup_w(nc.vector.tensor_copy, piece, 0, VECTOR_COLUMNS)
+                else:
+                    regroup_w(nc.scalar.copy, piece, 0, PIECE)
 
-        def vector_share(piece):
-            regroup_w(nc.vector.tensor_copy, piece, 0, VECTOR_COLUMNS)
-
-        def quantise_w(piece):
-            i, g, q = piece
+        def quantise_w(i, q):
             cols = slice(q * PIECE, (q + 1) * PIECE)
-            nc.vector.quantize_mx(
-                out=w_codes[:, i, g, cols].bitcast(FP8X4),
-                scales=w_scales[:, i, g, cols],
-                in_=w_grouped[piece][:].rearrange("p n t -> p (n t)"),
-            )
+            for g in range(PASSES):
+                nc.vector.quantize_mx(
+                    out=w_codes[:, i, g, cols].bitcast(FP8X4),
+                    scales=w_scales[:, i, g, cols],
+                    in_=w_grouped[i, g, q][:].rearrange("p n t -> p (n t)"),
+                )
 
-        def turn_x(i, batch):
+        def turn_x(i, batch, head=False):
             grouped = x_grouped_pool.tile([P, PASSES, TILES, P * PACK], BF16, align_bytes=64)
             x_grouped[i, batch] = grouped
             for m in range(TILES):
                 words = x_raw[i, batch][:].bitcast(F32)[:, m, :].rearrange(
                     "r (g p u) -> r g u p", g=PASSES, u=2
                 )
-                turned = turn_psum.tile([P, PASSES * 2, P], F32, tag="turn")
+                if head and m % 2 == 1:
+                    turned = back_psum.tile([P, PASSES * 2, P], F32, name="turned", tag="back")
+                else:
+                    turned = turn_psum.tile([P, PASSES * 2, P], F32, name="turned", tag="turn")
                 for g in range(PASSES):
                     for u in range(2):
                         nc.tensor.transpose(turned[:, 2 * g + u, :], words[:, g, u, :], ident[:])
@@ -135,11 +139,10 @@ def tile_crossmultiheadattention_pa_kernel(
                 in_=x_grouped[i, batch][:].rearrange("p g m c -> p (g m c)"),
             )
 
-        def project(i, r):
-            batch, head = divmod(r, HEADS)
+        def project_features(i, r):
+            batch, head = ORDER[r]
             features = slice(head * DH, (head + 1) * DH)
-            pool = ahead_psum if i == 0 else single_psum
-            bank = pool.tile([P, SEQ], F32, name="p_%d" % i, tag="p_%d" % i)
+            bank = product_psum.tile([P, SEQ], F32, name="p_%d" % i, tag="p_%d" % i)
             banks[i, r] = bank
             for g in range(PASSES):
                 tokens = slice(g * SEQ, (g + 1) * SEQ)
@@ -153,37 +156,78 @@ def tile_crossmultiheadattention_pa_kernel(
                     stop=(g == PASSES - 1),
                 )
 
+        def project_tokens(i, r):
+            batch, head = ORDER[r]
+            features = slice(head * DH, (head + 1) * DH)
+            bank = product_psum.tile([P, TILES, DH], F32, name="p_%d" % i, tag="p_%d" % i)
+            banks[i, r] = bank
+            for m in range(TILES):
+                for g in range(PASSES):
+                    tokens = slice(g * SEQ + m * P, g * SEQ + (m + 1) * P)
+                    nc.tensor.matmul_mx(
+                        out=bank[:, m, :],
+                        lhsT=x_codes[:, i, batch, tokens].bitcast(FP8X4),
+                        lhsT_scale=x_scales[:, i, batch, tokens],
+                        rhs=w_codes[:, i, g, features].bitcast(FP8X4),
+                        rhs_scale=w_scales[:, i, g, features],
+                        start=(g == 0),
+                        stop=(g == PASSES - 1),
+                    )
+
         def begin_mix(r):
-            head = r % HEADS
+            head = ORDER[r][1]
             mixes[r] = mix_pool.tile([P, NS, SEQ], F32, name="mix")
+            product = copied_pool.tile([P, SEQ], F32, name="product")
+            nc.scalar.copy(out=product[:], in_=banks[0, r][:])
             for j in range(NS):
-                nc.scalar.activation(
-                    out=mixes[r][:, j, :], in_=banks[0, r][:], func=IDENTITY,
-                    scale=w_scalar[:, j : j + 1], bias=bias_mix[:, j, head : head + 1],
+                nc.gpsimd.tensor_scalar(
+                    out=mixes[r][:, j, :], in0=product[:],
+                    scalar1=w_scalar[:, j : j + 1], scalar2=bias_mix[:, j, head : head + 1],
+                    op0=MULT, op1=ADD,
                 )
 
-        def add_stream(i, r):
+        def add_stream_1(r):
             for j in range(NS):
-                nc.vector.scalar_tensor_tensor(
-                    out=mixes[r][:, j, :], in0=banks[i, r][:],
-                    scalar=w_scalar[:, NS * i + j : NS * i + j + 1], in1=mixes[r][:, j, :],
-                    op0=MULT, op1=ADD,
+                if j not in scalar_outputs(r):
+                    nc.vector.scalar_tensor_tensor(
+                        out=mixes[r][:, j, :], in0=banks[1, r][:],
+                        scalar=w_scalar[:, NS + j : NS + j + 1], in1=mixes[r][:, j, :],
+                        op0=MULT, op1=ADD,
+                    )
+            for j in scalar_outputs(r):
+                terms[j, r] = term_pool.tile([P, SEQ], F32, name="term")
+                nc.scalar.activation(
+                    out=terms[j, r][:], in_=banks[1, r][:], func=IDENTITY,
+                    scale=w_scalar[:, NS + j : NS + j + 1],
                 )
 
         def turn_back(r):
             for j in range(NS):
-                turned_back[j, r] = turn_psum.tile([P, TILES, DH], F32, name="back", tag="turn")
+                turned_back[j, r] = back_psum.tile([P, TILES, DH], F32, name="back", tag="back")
+                parts = [mixes[r][:, j, :]]
+                if j in scalar_outputs(r):
+                    parts.append(terms[j, r][:])
                 for m in range(TILES):
-                    nc.tensor.transpose(
-                        turned_back[j, r][:, m, :], mixes[r][:, j, m * P : (m + 1) * P], ident[:]
-                    )
+                    for n, part in enumerate(parts):
+                        nc.tensor.matmul(
+                            turned_back[j, r][:, m, :], lhsT=part[:, m * P : (m + 1) * P],
+                            rhs=ident[:], is_transpose=True,
+                            start=(n == 0), stop=(n == len(parts) - 1),
+                        )
 
-        def store(r):
-            batch, head = divmod(r, HEADS)
+        def copy_stream_2(r):
+            copied[r] = copied_pool.tile([P, SEQ], F32, name="copied")
+            nc.scalar.copy(out=copied[r][:], in_=banks[2, r][:].rearrange("p m c -> p (m c)"))
+
+        def finish(r):
+            batch, head = ORDER[r]
             result = out_pool.tile([P, NS, SEQ], F32)
             for j in range(NS):
-                nc.scalar.copy(
-                    out=result[:, j, :], in_=turned_back[j, r][:].rearrange("p m c -> p (m c)")
+                nc.vector.scalar_tensor_tensor(
+                    out=result[:, j, :], in0=copied[r][:],
+                    scalar=w_scalar[:, 2 * NS + j : 2 * NS + j + 1],
+                    in1=turned_back[j, r][:].rearrange("p m c -> p (m c)"),
+                    op0=MULT, op1=ADD,
                 )
                 nc.sync.dma_start(
                     out=outs[j][batch, head].rearrange("(p m) c -> p (m c)", m=TILES),
@@ -207,12 +251,16 @@ def tile_crossmultiheadattention_pa_kernel(
 
         for i in range(NS):
             load_x(i, 0)
-            for g in range(PASSES):
-                load_w((i, g, 0))
-        for r in range(LOAD_AHEAD):
-            load_for(r)
+            load_w(i, 0)
+        for i in range(NS):
+            load_w(i, 1)
+        load_x(0, 1)
 
         nc.vector.tensor_copy(out=w_scalar[:], in_=w_bf16[:])
+        ctx.enter_context(tc.manual_schedule())
+
+        turn_x(0, 0, head=True)
+        group_w(0, 0)
         bias_f32 = keep.tile([P, P], F32)
         nc.vector.tensor_copy(out=bias_f32[:], in_=bias_rows[:])
         bias_cols = turn_psum.tile([P, P], F32, tag="turn")
@@ -229,49 +277,60 @@ def tile_crossmultiheadattention_pa_kernel(
                     scalar=w_scalar[:, NS * i + j : NS * i + j + 1], in1=bias_mix[:, j, :],
                     op0=MULT, op1=ADD,
                 )
-
-        ctx.enter_context(tc.manual_schedule())
-
-        turn_x(0, 0)
-        for i in range(NS):
-            for g in range(PASSES):
-                scalar_share((i, g, 0))
-                vector_share((i, g, 0))
-            if i + 1 < NS:
-                turn_x(i + 1, 0)
-            quantise_x(i, 0)
-            for g in range(PASSES):
-                quantise_w((i, g, 0))
-            project(i, 0)
+        quantise_x(0, 0)
+        turn_x(1, 0, head=True)
+        quantise_w(0, 0)
+        project_features(0, 0)
+        group_w(1, 0)
+        quantise_x(1, 0)
         begin_mix(0)
-        project(0, 1)
+        turn_x(2, 0, head=True)
+        quantise_w(1, 0)
+        project_features(1, 0)
+        project_features(0, 1)
+        add_stream_1(0)
+        group_w(2, 0)
+        begin_mix(1)
+        quantise_x(2, 0)
+        project_features(1, 1)
+        group_w(0, 1)
+        quantise_w(2, 0)
+        project_tokens(2, 0)
+        quantise_w(0, 1)
+        copy_stream_2(0)
+        project_features(0, 2)
+        group_w(1, 1)
 
         for r in range(ROUNDS):
-            pieces = pieces_of(r)
-            load_for(r + LOAD_AHEAD)
-            if r >= 1:
-                turn_back(r - 1)
-            for piece in pieces:
-                scalar_share(piece)
-            if r + 1 < ROUNDS:
-                begin_mix(r + 1)
-            if r >= 1:
-                store(r - 1)
-            add_stream(1, r)
-            for piece in pieces:
-                vector_share(piece)
-            if 0 <= r - X_TURN_ROUND - 1 < NS:
-                quantise_x(r - X_TURN_ROUND - 1, 1)
-            for piece in pieces:
-                quantise_w(piece)
-            if 0 <= r - X_TURN_ROUND < NS:
-                turn_x(r - X_TURN_ROUND, 1)
-            add_stream(2, r)
-            if r + 1 < ROUNDS:
-                project(1, r + 1)
+            if r + 1 in (1, 2):
+                load_x(r + 1, 1)
+            for q in (2, 3):
+                if r == 2 * q - 2:
+                    for i in range(NS):
+                        load_w(i, q)
+            turn_back(r)
             if r + 2 < ROUNDS:
-                project(0, r + 2)
+                begin_mix(r + 2)
             if r + 1 < ROUNDS:
-                project(2, r + 1)
-        turn_back(ROUNDS - 1)
-        store(ROUNDS - 1)
+                add_stream_1(r + 1)
+            for (i, q), when in W_ROUND.items():
+                if when == r:
+                    quantise_w(i, q)
+            for i, when in X_ROUND.items():
+                if when == r:
+                    quantise_x(i, 1)
+            if r + 1 < ROUNDS:
+                project_tokens(2, r + 1)
+            if r + 2 < ROUNDS:
+                project_features(1, r + 2)
+            if r + 3 < ROUNDS:
+                project_features(0, r + 3)
+            if r + 1 < ROUNDS:
+                copy_stream_2(r + 1)
+            for (i, q), when in W_ROUND.items():
+                if when == r + 1:
+                    group_w(i, q)
+            for i, when in X_ROUND.items():
+                if when == r + 1:
+                    turn_x(i, 1)
+            finish(r)

@@ -24,13 +24,20 @@ RUN = 4
 VECTOR_COLUMNS = 160
 ORDER = [(b, h) for first, last in ((0, 4), (4, 6), (6, 8)) for b in range(BATCH) for h in range(first, last)]
 ROUNDS = len(ORDER)
-W_ROUND = {(0, 1): -1, (1, 1): 0, (2, 1): 1, (0, 2): 4, (1, 2): 5, (2, 2): 6, (0, 3): 8, (1, 3): 9, (2, 3): 10}
-X_ROUND = {0: 1, 1: 2, 2: 3}
+W_ROUND = {(0, 1): -2, (1, 1): -1, (2, 1): 0, (0, 2): 3, (1, 2): 4, (2, 2): 5, (0, 3): 7, (1, 3): 8, (2, 3): 9}
+X_ROUND = {0: 0, 1: 1, 2: 2}
 
 
 def scalar_outputs(r):
-    return range(NS - (0 if r < 4 else 1 if r < 11 else 2), NS)
+    return range(NS - (1 if r >= 4 else 0), NS)
 
+
+HEAD_VECTOR = [(0, 1), (0, 3)]
+LATER_TILES = [(i, m) for i in range(NS) for m in range(TILES)]
+
+SCALAR_BEGINS = 2
+LATER_VECTOR = []
+REGROUP = {1: "VS", 2: "SS", 3: "SS"}
 
 FLOPS = 2 * NS * BATCH * SEQ * D * D
 
@@ -48,15 +55,15 @@ def tile_crossmultiheadattention_pa_kernel(
     with ExitStack() as ctx:
         keep = ctx.enter_context(tc.tile_pool(name="keep", bufs=1))
         x_raw_pool = ctx.enter_context(tc.tile_pool(name="x_raw", bufs=4))
+        w_raw_pool = ctx.enter_context(tc.tile_pool(name="w_raw", bufs=16))
         x_grouped_pool = ctx.enter_context(tc.tile_pool(name="x_grouped", bufs=2))
         w_grouped_pool = ctx.enter_context(tc.tile_pool(name="w_grouped", bufs=6))
-        mix_pool = ctx.enter_context(tc.tile_pool(name="mix", bufs=4))
-        term_pool = ctx.enter_context(tc.tile_pool(name="term", bufs=3))
+        mix_pool = ctx.enter_context(tc.tile_pool(name="mix", bufs=5))
+        term_pool = ctx.enter_context(tc.tile_pool(name="term", bufs=6))
         copied_pool = ctx.enter_context(tc.tile_pool(name="copied", bufs=3))
         out_pool = ctx.enter_context(tc.tile_pool(name="out", bufs=4))
         product_psum = ctx.enter_context(tc.psum_pool(name="product_psum", bufs=1))
-        back_psum = ctx.enter_context(tc.psum_pool(name="back_psum", bufs=3))
-        turn_psum = ctx.enter_context(tc.psum_pool(name="turn_psum", bufs=2))
+        turn_psum = ctx.enter_context(tc.psum_pool(name="turn_psum", bufs=5))
 
         x_codes = keep.tile([P, NS, BATCH, PASSES * SEQ], U32, align_bytes=64)
         x_scales = keep.tile([P, NS, BATCH, PASSES * SEQ], U8, align_bytes=64)
@@ -81,16 +88,21 @@ def tile_crossmultiheadattention_pa_kernel(
 
         def load_w(i, q):
             for g in range(PASSES):
-                tile = keep.tile([P, PACK, PIECE], BF16, name="w_raw_%d_%d_%d" % (i, g, q))
+                tile = w_raw_pool.tile([P, PACK, PIECE], BF16, name="w_raw")
                 w_raw[i, g, q] = tile
                 rows = weights[i][g * K_PASS : (g + 1) * K_PASS, q * PIECE : (q + 1) * PIECE]
-                nc.sync.dma_start(out=tile[:], in_=rows.rearrange("(p t) n -> p t n", t=PACK))
+                rows = rows.rearrange("(u p e) n -> u p e n", u=2, e=2)
+                for u in range(2):
+                    nc.sync.dma_start(out=tile[:, 2 * u : 2 * u + 2, :], in_=rows[u])
 
         def regroup_w(copy, piece, first, last):
             copy(
                 out=w_grouped[piece][:, first:last, :].rearrange("p (c r) t -> p c t r", r=RUN),
                 in_=w_raw[piece][:, :, first:last].rearrange("p t (c r) -> p c t r", r=RUN),
             )
+
+        def gpsimd_copy(out, in_):
+            nc.gpsimd.tensor_scalar(out=out, in0=in_, scalar1=1.0, scalar2=0.0, op0=MULT, op1=ADD)
 
         def group_w(i, q):
             for g in range(PASSES):
@@ -102,7 +114,7 @@ def tile_crossmultiheadattention_pa_kernel(
                     regroup_w(nc.scalar.copy, piece, VECTOR_COLUMNS, PIECE)
                     regroup_w(nc.vector.tensor_copy, piece, 0, VECTOR_COLUMNS)
                 else:
-                    regroup_w(nc.scalar.copy, piece, 0, PIECE)
+                    regroup_w({"S": nc.scalar.copy, "G": gpsimd_copy, "V": nc.vector.tensor_copy}[REGROUP[q][g]], piece, 0, PIECE)
 
         def quantise_w(i, q):
             cols = slice(q * PIECE, (q + 1) * PIECE)
@@ -113,24 +125,35 @@ def tile_crossmultiheadattention_pa_kernel(
                     in_=w_grouped[i, g, q][:].rearrange("p n t -> p (n t)"),
                 )
 
-        def turn_x(i, batch, head=False):
-            grouped = x_grouped_pool.tile([P, PASSES, TILES, P * PACK], BF16, align_bytes=64)
-            x_grouped[i, batch] = grouped
+        def turn_x(i, batch, m, copy):
+            if m == 0:
+                x_grouped[i, batch] = x_grouped_pool.tile(
+                    [P, PASSES, TILES, P * PACK], BF16, name="x_grouped", align_bytes=64
+                )
+            words = x_raw[i, batch][:].bitcast(F32)[:, m, :].rearrange(
+                "r (g u p) -> r g u p", g=PASSES, u=2
+            )
+            turned = turn_psum.tile([P, PASSES * 2, P], F32, name="turned", tag="turn")
+            for g in range(PASSES):
+                for u in range(2):
+                    nc.tensor.transpose(turned[:, 2 * g + u, :], words[:, g, u, :], ident[:])
+            copy(
+                out=x_grouped[i, batch][:].bitcast(F32)[:, :, m, :].rearrange(
+                    "p g (r u) -> p g r u", u=2
+                ),
+                in_=turned[:].rearrange("p (g u) r -> p g r u", u=2),
+            )
+
+        def turn_head(i):
             for m in range(TILES):
-                words = x_raw[i, batch][:].bitcast(F32)[:, m, :].rearrange(
-                    "r (g p u) -> r g u p", g=PASSES, u=2
+                turn_x(
+                    i, 0, m,
+                    nc.vector.tensor_copy if (i, m) in HEAD_VECTOR else nc.scalar.copy,
                 )
-                if head and m % 2 == 1:
-                    turned = back_psum.tile([P, PASSES * 2, P], F32, name="turned", tag="back")
-                else:
-                    turned = turn_psum.tile([P, PASSES * 2, P], F32, name="turned", tag="turn")
-                for g in range(PASSES):
-                    for u in range(2):
-                        nc.tensor.transpose(turned[:, 2 * g + u, :], words[:, g, u, :], ident[:])
-                nc.scalar.copy(
-                    out=grouped[:].bitcast(F32)[:, :, m, :].rearrange("p g (r u) -> p g r u", u=2),
-                    in_=turned[:].rearrange("p (g u) r -> p g r u", u=2),
-                )
+
+        def turn_later(n):
+            for i, m in LATER_TILES[2 * n : 2 * n + 2]:
+                turn_x(i, 1, m, nc.vector.tensor_copy if (i, m) in LATER_VECTOR else nc.scalar.copy)
 
         def quantise_x(i, batch):
             nc.vector.quantize_mx(
@@ -177,6 +200,13 @@ def tile_crossmultiheadattention_pa_kernel(
         def begin_mix(r):
             head = ORDER[r][1]
             mixes[r] = mix_pool.tile([P, NS, SEQ], F32, name="mix")
+            if r < SCALAR_BEGINS:
+                for j in range(NS):
+                    nc.scalar.activation(
+                        out=mixes[r][:, j, :], in_=banks[0, r][:], func=IDENTITY,
+                        scale=w_scalar[:, j : j + 1], bias=bias_mix[:, j, head : head + 1],
+                    )
+                return
             product = copied_pool.tile([P, SEQ], F32, name="product")
             nc.scalar.copy(out=product[:], in_=banks[0, r][:])
             for j in range(NS):
@@ -194,6 +224,8 @@ def tile_crossmultiheadattention_pa_kernel(
                         scalar=w_scalar[:, NS + j : NS + j + 1], in1=mixes[r][:, j, :],
                         op0=MULT, op1=ADD,
                     )
+
+        def make_terms(r):
             for j in scalar_outputs(r):
                 terms[j, r] = term_pool.tile([P, SEQ], F32, name="term")
                 nc.scalar.activation(
@@ -203,7 +235,7 @@ def tile_crossmultiheadattention_pa_kernel(
 
         def turn_back(r):
             for j in range(NS):
-                turned_back[j, r] = back_psum.tile([P, TILES, DH], F32, name="back", tag="back")
+                turned_back[j, r] = turn_psum.tile([P, TILES, DH], F32, name="back", tag="turn")
                 parts = [mixes[r][:, j, :]]
                 if j in scalar_outputs(r):
                     parts.append(terms[j, r][:])
@@ -252,15 +284,23 @@ def tile_crossmultiheadattention_pa_kernel(
         for i in range(NS):
             load_x(i, 0)
             load_w(i, 0)
-        for i in range(NS):
-            load_w(i, 1)
+        load_w(0, 1)
         load_x(0, 1)
+        load_w(1, 1)
 
         nc.vector.tensor_copy(out=w_scalar[:], in_=w_bf16[:])
         ctx.enter_context(tc.manual_schedule())
 
-        turn_x(0, 0, head=True)
+        turn_head(0)
         group_w(0, 0)
+        quantise_x(0, 0)
+        quantise_w(0, 0)
+        load_x(1, 1)
+        load_w(2, 1)
+        turn_head(1)
+        load_x(2, 1)
+        project_features(0, 0)
+        group_w(1, 0)
         bias_f32 = keep.tile([P, P], F32)
         nc.vector.tensor_copy(out=bias_f32[:], in_=bias_rows[:])
         bias_cols = turn_psum.tile([P, P], F32, tag="turn")
@@ -277,60 +317,61 @@ def tile_crossmultiheadattention_pa_kernel(
                     scalar=w_scalar[:, NS * i + j : NS * i + j + 1], in1=bias_mix[:, j, :],
                     op0=MULT, op1=ADD,
                 )
-        quantise_x(0, 0)
-        turn_x(1, 0, head=True)
-        quantise_w(0, 0)
-        project_features(0, 0)
-        group_w(1, 0)
         quantise_x(1, 0)
-        begin_mix(0)
-        turn_x(2, 0, head=True)
         quantise_w(1, 0)
+        begin_mix(0)
+        turn_head(2)
         project_features(1, 0)
         project_features(0, 1)
-        add_stream_1(0)
+        make_terms(0)
         group_w(2, 0)
-        begin_mix(1)
+        add_stream_1(0)
         quantise_x(2, 0)
-        project_features(1, 1)
-        group_w(0, 1)
+        begin_mix(1)
         quantise_w(2, 0)
         project_tokens(2, 0)
-        quantise_w(0, 1)
+        project_features(1, 1)
+        make_terms(1)
+        group_w(0, 1)
         copy_stream_2(0)
-        project_features(0, 2)
         group_w(1, 1)
+        quantise_w(0, 1)
+        turn_later(0)
+        project_features(0, 2)
+        begin_mix(2)
+        quantise_w(1, 1)
+        group_w(2, 1)
+        turn_later(1)
 
         for r in range(ROUNDS):
-            if r + 1 in (1, 2):
-                load_x(r + 1, 1)
             for q in (2, 3):
                 if r == 2 * q - 2:
                     for i in range(NS):
                         load_w(i, q)
             turn_back(r)
-            if r + 2 < ROUNDS:
-                begin_mix(r + 2)
+            if 0 <= r < 2:
+                turn_later(2 * r + 2)
             if r + 1 < ROUNDS:
                 add_stream_1(r + 1)
+            if r + 1 < ROUNDS:
+                project_tokens(2, r + 1)
+            if r + 2 < ROUNDS:
+                project_features(1, r + 2)
+                make_terms(r + 2)
+            if r + 3 < ROUNDS:
+                project_features(0, r + 3)
+                begin_mix(r + 3)
+            if r + 1 < ROUNDS:
+                copy_stream_2(r + 1)
+            finish(r)
             for (i, q), when in W_ROUND.items():
                 if when == r:
                     quantise_w(i, q)
             for i, when in X_ROUND.items():
                 if when == r:
                     quantise_x(i, 1)
-            if r + 1 < ROUNDS:
-                project_tokens(2, r + 1)
-            if r + 2 < ROUNDS:
-                project_features(1, r + 2)
-            if r + 3 < ROUNDS:
-                project_features(0, r + 3)
-            if r + 1 < ROUNDS:
-                copy_stream_2(r + 1)
             for (i, q), when in W_ROUND.items():
                 if when == r + 1:
                     group_w(i, q)
-            for i, when in X_ROUND.items():
-                if when == r + 1:
-                    turn_x(i, 1)
-            finish(r)
+            if 0 <= r < 2:
+                turn_later(2 * r + 3)

@@ -35,7 +35,7 @@ def scalar_outputs(r):
 HEAD_VECTOR = [(0, 1), (0, 3)]
 LATER_TILES = [(i, m) for i in range(NS) for m in range(TILES)]
 
-SCALAR_BEGINS = 2
+SCALAR_BEGINS = 1
 LATER_VECTOR = []
 REGROUP = {1: "VS", 2: "SS", 3: "SS"}
 
@@ -55,13 +55,13 @@ def tile_crossmultiheadattention_pa_kernel(
     with ExitStack() as ctx:
         keep = ctx.enter_context(tc.tile_pool(name="keep", bufs=1))
         x_raw_pool = ctx.enter_context(tc.tile_pool(name="x_raw", bufs=4))
-        w_raw_pool = ctx.enter_context(tc.tile_pool(name="w_raw", bufs=16))
+        w_raw_pool = ctx.enter_context(tc.tile_pool(name="w_raw", bufs=NS))
         x_grouped_pool = ctx.enter_context(tc.tile_pool(name="x_grouped", bufs=2))
         w_grouped_pool = ctx.enter_context(tc.tile_pool(name="w_grouped", bufs=6))
-        mix_pool = ctx.enter_context(tc.tile_pool(name="mix", bufs=5))
-        term_pool = ctx.enter_context(tc.tile_pool(name="term", bufs=6))
+        mix_pool = ctx.enter_context(tc.tile_pool(name="mix", bufs=4))
+        term_pool = ctx.enter_context(tc.tile_pool(name="term", bufs=3))
         copied_pool = ctx.enter_context(tc.tile_pool(name="copied", bufs=3))
-        out_pool = ctx.enter_context(tc.tile_pool(name="out", bufs=4))
+        out_pool = ctx.enter_context(tc.tile_pool(name="out", bufs=2))
         product_psum = ctx.enter_context(tc.psum_pool(name="product_psum", bufs=1))
         turn_psum = ctx.enter_context(tc.psum_pool(name="turn_psum", bufs=5))
 
@@ -78,22 +78,27 @@ def tile_crossmultiheadattention_pa_kernel(
         mixes = {}
         terms = {}
         copied = {}
+        results = {}
         turned_back = {}
 
         def load_x(i, batch):
             x_raw[i, batch] = x_raw_pool.tile([P, TILES, D], BF16, name="x_raw")
             rows = streams[i][batch].rearrange("(p m) k -> p m k", m=TILES)
-            for m in range(TILES):
-                nc.sync.dma_start(out=x_raw[i, batch][:, m, :], in_=rows[:, m, :])
+            for m in range(0, TILES, 2):
+                nc.sync.dma_start(out=x_raw[i, batch][:, m : m + 2, :], in_=rows[:, m : m + 2, :])
 
-        def load_w(i, q):
+        def load_w(i, first, last):
+            tile = w_raw_pool.tile(
+                [P, PASSES, PACK, (last - first) * PIECE], BF16, name="w_raw_%d_%d" % (first, last)
+            )
+            rows = weights[i][:, first * PIECE : last * PIECE].rearrange(
+                "(v p e) n -> v p e n", p=P, e=2
+            )
             for g in range(PASSES):
-                tile = w_raw_pool.tile([P, PACK, PIECE], BF16, name="w_raw")
-                w_raw[i, g, q] = tile
-                rows = weights[i][g * K_PASS : (g + 1) * K_PASS, q * PIECE : (q + 1) * PIECE]
-                rows = rows.rearrange("(u p e) n -> u p e n", u=2, e=2)
                 for u in range(2):
-                    nc.sync.dma_start(out=tile[:, 2 * u : 2 * u + 2, :], in_=rows[u])
+                    nc.sync.dma_start(out=tile[:, g, 2 * u : 2 * u + 2, :], in_=rows[2 * g + u])
+                for q in range(first, last):
+                    w_raw[i, g, q] = tile[:, g, :, (q - first) * PIECE : (q - first + 1) * PIECE]
 
         def regroup_w(copy, piece, first, last):
             copy(
@@ -253,18 +258,27 @@ def tile_crossmultiheadattention_pa_kernel(
 
         def finish(r):
             batch, head = ORDER[r]
-            result = out_pool.tile([P, NS, SEQ], F32)
+            half = r % 2
+            if half == 0:
+                results[r] = out_pool.tile([P, NS, 2, SEQ], F32, name="result")
+                results[r + 1] = results[r]
             for j in range(NS):
                 nc.vector.scalar_tensor_tensor(
-                    out=result[:, j, :], in0=copied[r][:],
+                    out=results[r][:, j, half, :], in0=copied[r][:],
                     scalar=w_scalar[:, 2 * NS + j : 2 * NS + j + 1],
                     in1=turned_back[j, r][:].rearrange("p m c -> p (m c)"),
                     op0=MULT, op1=ADD,
                 )
-                nc.sync.dma_start(
-                    out=outs[j][batch, head].rearrange("(p m) c -> p (m c)", m=TILES),
-                    in_=result[:, j, :],
-                )
+                if r >= ROUNDS - 2:
+                    nc.sync.dma_start(
+                        out=outs[j][batch, head].rearrange("(p m) c -> p (m c)", m=TILES),
+                        in_=results[r][:, j, half, :],
+                    )
+                elif half == 1:
+                    nc.sync.dma_start(
+                        out=outs[j][batch, head - 1 : head + 1].rearrange("h (p m) c -> p h (m c)", m=TILES),
+                        in_=results[r][:, j, :, :],
+                    )
 
         ident = keep.tile([P, P], F32)
         masks.make_identity(nc, ident[:])
@@ -283,20 +297,20 @@ def tile_crossmultiheadattention_pa_kernel(
 
         for i in range(NS):
             load_x(i, 0)
-            load_w(i, 0)
-        load_w(0, 1)
-        load_x(0, 1)
-        load_w(1, 1)
+            load_w(i, 0, 1)
 
         nc.vector.tensor_copy(out=w_scalar[:], in_=w_bf16[:])
         ctx.enter_context(tc.manual_schedule())
 
         turn_head(0)
+        load_w(0, 1, 2)
+        load_x(0, 1)
+        load_w(1, 1, 2)
         group_w(0, 0)
         quantise_x(0, 0)
         quantise_w(0, 0)
         load_x(1, 1)
-        load_w(2, 1)
+        load_w(2, 1, 2)
         turn_head(1)
         load_x(2, 1)
         project_features(0, 0)
@@ -344,10 +358,9 @@ def tile_crossmultiheadattention_pa_kernel(
         turn_later(1)
 
         for r in range(ROUNDS):
-            for q in (2, 3):
-                if r == 2 * q - 2:
-                    for i in range(NS):
-                        load_w(i, q)
+            if r == 1:
+                for i in range(NS):
+                    load_w(i, 2, 4)
             turn_back(r)
             if 0 <= r < 2:
                 turn_later(2 * r + 2)

@@ -20,6 +20,7 @@ DH = D // HEADS
 PASSES = D // K_PASS
 TILES = SEQ // P
 PIECE = 256
+QUARTERS = D // PIECE
 RUN = 4
 VECTOR_COLUMNS = 160
 ORDER = [(b, h) for first, last in ((0, 4), (4, 6), (6, 8)) for b in range(BATCH) for h in range(first, last)]
@@ -57,7 +58,7 @@ def tile_crossmultiheadattention_pa_kernel(
         x_raw_pool = ctx.enter_context(tc.tile_pool(name="x_raw", bufs=4))
         w_raw_pool = ctx.enter_context(tc.tile_pool(name="w_raw", bufs=NS))
         x_grouped_pool = ctx.enter_context(tc.tile_pool(name="x_grouped", bufs=2))
-        w_grouped_pool = ctx.enter_context(tc.tile_pool(name="w_grouped", bufs=6))
+        w_grouped_pool = ctx.enter_context(tc.tile_pool(name="w_grouped", bufs=3))
         mix_pool = ctx.enter_context(tc.tile_pool(name="mix", bufs=4))
         term_pool = ctx.enter_context(tc.tile_pool(name="term", bufs=3))
         copied_pool = ctx.enter_context(tc.tile_pool(name="copied", bufs=3))
@@ -67,8 +68,8 @@ def tile_crossmultiheadattention_pa_kernel(
 
         x_codes = keep.tile([P, NS, BATCH, PASSES * SEQ], U32, align_bytes=64)
         x_scales = keep.tile([P, NS, BATCH, PASSES * SEQ], U8, align_bytes=64)
-        w_codes = keep.tile([P, NS, PASSES, D], U32, align_bytes=64)
-        w_scales = keep.tile([P, NS, PASSES, D], U8, align_bytes=64)
+        w_codes = keep.tile([P, NS, QUARTERS, PASSES * PIECE], U32, align_bytes=64)
+        w_scales = keep.tile([P, NS, QUARTERS, PASSES * PIECE], U8, align_bytes=64)
 
         x_raw = {}
         x_grouped = {}
@@ -100,35 +101,36 @@ def tile_crossmultiheadattention_pa_kernel(
                 for q in range(first, last):
                     w_raw[i, g, q] = tile[:, g, :, (q - first) * PIECE : (q - first + 1) * PIECE]
 
-        def regroup_w(copy, piece, first, last):
+        def regroup_w(copy, i, g, q, first, last):
             copy(
-                out=w_grouped[piece][:, first:last, :].rearrange("p (c r) t -> p c t r", r=RUN),
-                in_=w_raw[piece][:, :, first:last].rearrange("p t (c r) -> p c t r", r=RUN),
+                out=w_grouped[i, q][:, g, first:last, :].rearrange("p (c r) t -> p c t r", r=RUN),
+                in_=w_raw[i, g, q][:, :, first:last].rearrange("p t (c r) -> p c t r", r=RUN),
             )
 
         def gpsimd_copy(out, in_):
             nc.gpsimd.tensor_scalar(out=out, in0=in_, scalar1=1.0, scalar2=0.0, op0=MULT, op1=ADD)
 
         def group_w(i, q):
+            w_grouped[i, q] = w_grouped_pool.tile(
+                [P, PASSES, PIECE, PACK], BF16, name="w_grouped", align_bytes=64
+            )
             for g in range(PASSES):
-                piece = (i, g, q)
-                w_grouped[piece] = w_grouped_pool.tile(
-                    [P, PIECE, PACK], BF16, name="w_grouped", align_bytes=64
-                )
                 if q == 0:
-                    regroup_w(nc.scalar.copy, piece, VECTOR_COLUMNS, PIECE)
-                    regroup_w(nc.vector.tensor_copy, piece, 0, VECTOR_COLUMNS)
+                    regroup_w(nc.scalar.copy, i, g, q, VECTOR_COLUMNS, PIECE)
+                    regroup_w(nc.vector.tensor_copy, i, g, q, 0, VECTOR_COLUMNS)
                 else:
-                    regroup_w({"S": nc.scalar.copy, "G": gpsimd_copy, "V": nc.vector.tensor_copy}[REGROUP[q][g]], piece, 0, PIECE)
+                    regroup_w({"S": nc.scalar.copy, "G": gpsimd_copy, "V": nc.vector.tensor_copy}[REGROUP[q][g]], i, g, q, 0, PIECE)
 
         def quantise_w(i, q):
-            cols = slice(q * PIECE, (q + 1) * PIECE)
-            for g in range(PASSES):
-                nc.vector.quantize_mx(
-                    out=w_codes[:, i, g, cols].bitcast(FP8X4),
-                    scales=w_scales[:, i, g, cols],
-                    in_=w_grouped[i, g, q][:].rearrange("p n t -> p (n t)"),
-                )
+            nc.vector.quantize_mx(
+                out=w_codes[:, i, q, :].bitcast(FP8X4),
+                scales=w_scales[:, i, q, :],
+                in_=w_grouped[i, q][:].rearrange("p g n t -> p (g n t)"),
+            )
+
+        def w_slice(head, g):
+            first = g * PIECE + head % (PIECE // DH) * DH
+            return slice(first, first + DH)
 
         def turn_x(i, batch, m, copy):
             if m == 0:
@@ -169,15 +171,15 @@ def tile_crossmultiheadattention_pa_kernel(
 
         def project_features(i, r):
             batch, head = ORDER[r]
-            features = slice(head * DH, (head + 1) * DH)
+            q = head * DH // PIECE
             bank = product_psum.tile([P, SEQ], F32, name="p_%d" % i, tag="p_%d" % i)
             banks[i, r] = bank
             for g in range(PASSES):
                 tokens = slice(g * SEQ, (g + 1) * SEQ)
                 nc.tensor.matmul_mx(
                     out=bank[:],
-                    lhsT=w_codes[:, i, g, features].bitcast(FP8X4),
-                    lhsT_scale=w_scales[:, i, g, features],
+                    lhsT=w_codes[:, i, q, w_slice(head, g)].bitcast(FP8X4),
+                    lhsT_scale=w_scales[:, i, q, w_slice(head, g)],
                     rhs=x_codes[:, i, batch, tokens].bitcast(FP8X4),
                     rhs_scale=x_scales[:, i, batch, tokens],
                     start=(g == 0),
@@ -186,7 +188,7 @@ def tile_crossmultiheadattention_pa_kernel(
 
         def project_tokens(i, r):
             batch, head = ORDER[r]
-            features = slice(head * DH, (head + 1) * DH)
+            q = head * DH // PIECE
             bank = product_psum.tile([P, TILES, DH], F32, name="p_%d" % i, tag="p_%d" % i)
             banks[i, r] = bank
             for m in range(TILES):
@@ -196,8 +198,8 @@ def tile_crossmultiheadattention_pa_kernel(
                         out=bank[:, m, :],
                         lhsT=x_codes[:, i, batch, tokens].bitcast(FP8X4),
                         lhsT_scale=x_scales[:, i, batch, tokens],
-                        rhs=w_codes[:, i, g, features].bitcast(FP8X4),
-                        rhs_scale=w_scales[:, i, g, features],
+                        rhs=w_codes[:, i, q, w_slice(head, g)].bitcast(FP8X4),
+                        rhs_scale=w_scales[:, i, q, w_slice(head, g)],
                         start=(g == 0),
                         stop=(g == PASSES - 1),
                     )

@@ -14,33 +14,42 @@ IDENTITY = mybir.ActivationFunctionType.Identity
 
 P = 128
 PACK = 4
-K_PASS = P * PACK
 BATCH, SEQ, D, HEADS, NS = 2, 512, 1024, 8, 3
 DH = D // HEADS
-PASSES = D // K_PASS
-TILES = SEQ // P
-PIECE = 256
+PASSES = D // (P * PACK)
+HALVES = 2
+TILES = SEQ // P // HALVES
+HALF = SEQ // HALVES
+PIECE = 2 * DH
 QUARTERS = D // PIECE
 RUN = 4
 VECTOR_COLUMNS = 160
-ORDER = [(b, h) for first, last in ((0, 4), (4, 6), (6, 8)) for b in range(BATCH) for h in range(first, last)]
+def whole(b, h):
+    return [(b, [h], [0, 1]), (b, [h + 1], [0, 1])]
+
+
+def halved(b, h):
+    return [(b, [h, h + 1], [0]), (b, [h, h + 1], [1])]
+
+
+ORDER = halved(0, 0) + whole(0, 2) + whole(0, 4) + halved(1, 0) + whole(1, 2) + whole(1, 4) + whole(0, 6) + whole(1, 6)
 ROUNDS = len(ORDER)
-W_ROUND = {(0, 1): -2, (1, 1): -1, (2, 1): 0, (0, 2): 3, (1, 2): 4, (2, 2): 5, (0, 3): 7, (1, 3): 8, (2, 3): 9}
-X_ROUND = {0: 0, 1: 1, 2: 2}
-
-
-def scalar_outputs(r):
-    return range(NS - (1 if r >= 4 else 0), NS)
-
-
-HEAD_VECTOR = [(0, 1), (0, 3)]
-LATER_TILES = [(i, m) for i in range(NS) for m in range(TILES)]
-
-SCALAR_BEGINS = 1
-LATER_VECTOR = []
+SCALAR_BEGINS = 3
+HEAD_VECTOR = [(0, 0, 1), (1, 0, 1), (2, 0, 1)]
+QUANTISE_W = {2: [(2, 2)], 8: [(0, 3)], 9: [(1, 3)], 10: [(2, 3)]}
+QW_EARLY = {2: [(1, 2)]}
+QUANTISE_X = {2: [(0, 0)], 3: [(1, 0), (0, 1)], 4: [(1, 1), (2, 0)], 5: [(2, 1)]}
+QX_EARLY = {}
+TURN_BEFORE = {2: [(0, 0)], 3: [(0, 1)], 4: [(2, 0)]}
+TURN_AFTER = {2: [(1, 0)], 3: [(1, 1)], 4: [(2, 1)]}
+REGROUP_W = {7: [(0, 3)], 8: [(1, 3)], 9: [(2, 3)]}
 REGROUP = {1: "VS", 2: "SS", 3: "SS"}
 
 FLOPS = 2 * NS * BATCH * SEQ * D * D
+
+
+def scalar_outputs(r):
+    return range(NS - (1 if r >= 6 else 0), NS)
 
 
 def tile_crossmultiheadattention_pa_kernel(
@@ -55,19 +64,19 @@ def tile_crossmultiheadattention_pa_kernel(
 
     with ExitStack() as ctx:
         keep = ctx.enter_context(tc.tile_pool(name="keep", bufs=1))
-        x_raw_pool = ctx.enter_context(tc.tile_pool(name="x_raw", bufs=4))
+        x_raw_pool = ctx.enter_context(tc.tile_pool(name="x_raw", bufs=7))
         w_raw_pool = ctx.enter_context(tc.tile_pool(name="w_raw", bufs=NS))
-        x_grouped_pool = ctx.enter_context(tc.tile_pool(name="x_grouped", bufs=2))
+        x_grouped_pool = ctx.enter_context(tc.tile_pool(name="x_grouped", bufs=4))
         w_grouped_pool = ctx.enter_context(tc.tile_pool(name="w_grouped", bufs=3))
-        mix_pool = ctx.enter_context(tc.tile_pool(name="mix", bufs=4))
+        mix_pool = ctx.enter_context(tc.tile_pool(name="mix", bufs=5))
         term_pool = ctx.enter_context(tc.tile_pool(name="term", bufs=3))
         copied_pool = ctx.enter_context(tc.tile_pool(name="copied", bufs=3))
         out_pool = ctx.enter_context(tc.tile_pool(name="out", bufs=2))
         product_psum = ctx.enter_context(tc.psum_pool(name="product_psum", bufs=1))
         turn_psum = ctx.enter_context(tc.psum_pool(name="turn_psum", bufs=5))
 
-        x_codes = keep.tile([P, NS, BATCH, PASSES * SEQ], U32, align_bytes=64)
-        x_scales = keep.tile([P, NS, BATCH, PASSES * SEQ], U8, align_bytes=64)
+        x_codes = keep.tile([P, NS, BATCH, HALVES, PASSES * HALF], U32, align_bytes=64)
+        x_scales = keep.tile([P, NS, BATCH, HALVES, PASSES * HALF], U8, align_bytes=64)
         w_codes = keep.tile([P, NS, QUARTERS, PASSES * PIECE], U32, align_bytes=64)
         w_scales = keep.tile([P, NS, QUARTERS, PASSES * PIECE], U8, align_bytes=64)
 
@@ -82,11 +91,12 @@ def tile_crossmultiheadattention_pa_kernel(
         results = {}
         turned_back = {}
 
-        def load_x(i, batch):
-            x_raw[i, batch] = x_raw_pool.tile([P, TILES, D], BF16, name="x_raw")
-            rows = streams[i][batch].rearrange("(p m) k -> p m k", m=TILES)
-            for m in range(0, TILES, 2):
-                nc.sync.dma_start(out=x_raw[i, batch][:, m : m + 2, :], in_=rows[:, m : m + 2, :])
+        def load_x(i, batch, half):
+            x_raw[i, batch, half] = x_raw_pool.tile([P, TILES, D], BF16, name="x_raw")
+            rows = streams[i][batch].rearrange("(p m) k -> p m k", p=P)
+            nc.sync.dma_start(
+                out=x_raw[i, batch, half][:], in_=rows[:, half * TILES : (half + 1) * TILES, :]
+            )
 
         def load_w(i, first, last):
             tile = w_raw_pool.tile(
@@ -128,100 +138,94 @@ def tile_crossmultiheadattention_pa_kernel(
                 in_=w_grouped[i, q][:].rearrange("p g n t -> p (g n t)"),
             )
 
-        def w_slice(head, g):
-            first = g * PIECE + head % (PIECE // DH) * DH
-            return slice(first, first + DH)
+        def w_columns(head, g, count):
+            first = g * PIECE + head % 2 * DH
+            return slice(first, first + count * DH)
 
-        def turn_x(i, batch, m, copy):
-            if m == 0:
-                x_grouped[i, batch] = x_grouped_pool.tile(
-                    [P, PASSES, TILES, P * PACK], BF16, name="x_grouped", align_bytes=64
-                )
-            words = x_raw[i, batch][:].bitcast(F32)[:, m, :].rearrange(
-                "r (g u p) -> r g u p", g=PASSES, u=2
-            )
-            turned = turn_psum.tile([P, PASSES * 2, P], F32, name="turned", tag="turn")
-            for g in range(PASSES):
-                for u in range(2):
-                    nc.tensor.transpose(turned[:, 2 * g + u, :], words[:, g, u, :], ident[:])
-            copy(
-                out=x_grouped[i, batch][:].bitcast(F32)[:, :, m, :].rearrange(
-                    "p g (r u) -> p g r u", u=2
-                ),
-                in_=turned[:].rearrange("p (g u) r -> p g r u", u=2),
-            )
+        def x_columns(g, first, count):
+            return slice(g * HALF + first * P, g * HALF + (first + count) * P)
 
-        def turn_head(i):
+        def turn_x(i, batch, half):
+            x_grouped[i, batch, half] = x_grouped_pool.tile(
+                [P, PASSES, TILES, P * PACK], BF16, name="x_grouped", align_bytes=64
+            )
             for m in range(TILES):
-                turn_x(
-                    i, 0, m,
-                    nc.vector.tensor_copy if (i, m) in HEAD_VECTOR else nc.scalar.copy,
+                words = x_raw[i, batch, half][:].bitcast(F32)[:, m, :].rearrange(
+                    "r (g u p) -> r g u p", g=PASSES, u=2
+                )
+                turned = turn_psum.tile([P, PASSES * 2, P], F32, name="turned", tag="turn")
+                for g in range(PASSES):
+                    for u in range(2):
+                        nc.tensor.transpose(turned[:, 2 * g + u, :], words[:, g, u, :], ident[:])
+                copy = nc.vector.tensor_copy if batch == 0 and (i, half, m) in HEAD_VECTOR else nc.scalar.copy
+                copy(
+                    out=x_grouped[i, batch, half][:].bitcast(F32)[:, :, m, :].rearrange(
+                        "p g (r u) -> p g r u", u=2
+                    ),
+                    in_=turned[:].rearrange("p (g u) r -> p g r u", u=2),
                 )
 
-        def turn_later(n):
-            for i, m in LATER_TILES[2 * n : 2 * n + 2]:
-                turn_x(i, 1, m, nc.vector.tensor_copy if (i, m) in LATER_VECTOR else nc.scalar.copy)
-
-        def quantise_x(i, batch):
+        def quantise_x(i, batch, half):
             nc.vector.quantize_mx(
-                out=x_codes[:, i, batch, :].bitcast(FP8X4),
-                scales=x_scales[:, i, batch, :],
-                in_=x_grouped[i, batch][:].rearrange("p g m c -> p (g m c)"),
+                out=x_codes[:, i, batch, half, :].bitcast(FP8X4),
+                scales=x_scales[:, i, batch, half, :],
+                in_=x_grouped[i, batch, half][:].rearrange("p g m c -> p (g m c)"),
             )
 
         def project_features(i, r):
-            batch, head = ORDER[r]
-            q = head * DH // PIECE
+            batch, heads, halves = ORDER[r]
             bank = product_psum.tile([P, SEQ], F32, name="p_%d" % i, tag="p_%d" % i)
             banks[i, r] = bank
-            for g in range(PASSES):
-                tokens = slice(g * SEQ, (g + 1) * SEQ)
-                nc.tensor.matmul_mx(
-                    out=bank[:],
-                    lhsT=w_codes[:, i, q, w_slice(head, g)].bitcast(FP8X4),
-                    lhsT_scale=w_scales[:, i, q, w_slice(head, g)],
-                    rhs=x_codes[:, i, batch, tokens].bitcast(FP8X4),
-                    rhs_scale=x_scales[:, i, batch, tokens],
-                    start=(g == 0),
-                    stop=(g == PASSES - 1),
-                )
+            for n, (head, half) in enumerate([(head, half) for head in heads for half in halves]):
+                for g in range(PASSES):
+                    nc.tensor.matmul_mx(
+                        out=bank[:, n * HALF : (n + 1) * HALF],
+                        lhsT=w_codes[:, i, head // 2, w_columns(head, g, 1)].bitcast(FP8X4),
+                        lhsT_scale=w_scales[:, i, head // 2, w_columns(head, g, 1)],
+                        rhs=x_codes[:, i, batch, half, x_columns(g, 0, TILES)].bitcast(FP8X4),
+                        rhs_scale=x_scales[:, i, batch, half, x_columns(g, 0, TILES)],
+                        start=(g == 0),
+                        stop=(g == PASSES - 1),
+                    )
 
         def project_tokens(i, r):
-            batch, head = ORDER[r]
-            q = head * DH // PIECE
-            bank = product_psum.tile([P, TILES, DH], F32, name="p_%d" % i, tag="p_%d" % i)
+            batch, heads, halves = ORDER[r]
+            bank = product_psum.tile([P, SEQ], F32, name="p_%d" % i, tag="p_%d" % i)
             banks[i, r] = bank
-            for m in range(TILES):
+            blocks = [(head, half, m) for head in heads for half in halves for m in range(TILES)]
+            for n, (head, half, m) in enumerate(blocks):
                 for g in range(PASSES):
-                    tokens = slice(g * SEQ + m * P, g * SEQ + (m + 1) * P)
                     nc.tensor.matmul_mx(
-                        out=bank[:, m, :],
-                        lhsT=x_codes[:, i, batch, tokens].bitcast(FP8X4),
-                        lhsT_scale=x_scales[:, i, batch, tokens],
-                        rhs=w_codes[:, i, q, w_slice(head, g)].bitcast(FP8X4),
-                        rhs_scale=w_scales[:, i, q, w_slice(head, g)],
+                        out=bank[:, n * P : (n + 1) * P],
+                        lhsT=x_codes[:, i, batch, half, x_columns(g, m, 1)].bitcast(FP8X4),
+                        lhsT_scale=x_scales[:, i, batch, half, x_columns(g, m, 1)],
+                        rhs=w_codes[:, i, head // 2, w_columns(head, g, 1)].bitcast(FP8X4),
+                        rhs_scale=w_scales[:, i, head // 2, w_columns(head, g, 1)],
                         start=(g == 0),
                         stop=(g == PASSES - 1),
                     )
 
         def begin_mix(r):
-            head = ORDER[r][1]
+            heads = ORDER[r][1]
+            width = SEQ // len(heads)
             mixes[r] = mix_pool.tile([P, NS, SEQ], F32, name="mix")
-            if r < SCALAR_BEGINS:
-                for j in range(NS):
-                    nc.scalar.activation(
-                        out=mixes[r][:, j, :], in_=banks[0, r][:], func=IDENTITY,
-                        scale=w_scalar[:, j : j + 1], bias=bias_mix[:, j, head : head + 1],
-                    )
-                return
-            product = copied_pool.tile([P, SEQ], F32, name="product")
-            nc.scalar.copy(out=product[:], in_=banks[0, r][:])
+            if r >= SCALAR_BEGINS:
+                product = copied_pool.tile([P, SEQ], F32, name="product")
+                nc.scalar.copy(out=product[:], in_=banks[0, r][:])
             for j in range(NS):
-                nc.gpsimd.tensor_scalar(
-                    out=mixes[r][:, j, :], in0=product[:],
-                    scalar1=w_scalar[:, j : j + 1], scalar2=bias_mix[:, j, head : head + 1],
-                    op0=MULT, op1=ADD,
-                )
+                for n, head in enumerate(heads):
+                    columns = slice(n * width, (n + 1) * width)
+                    if r < SCALAR_BEGINS:
+                        nc.scalar.activation(
+                            out=mixes[r][:, j, columns], in_=banks[0, r][:, columns], func=IDENTITY,
+                            scale=w_scalar[:, j : j + 1], bias=bias_mix[:, j, head : head + 1],
+                        )
+                    else:
+                        nc.gpsimd.tensor_scalar(
+                            out=mixes[r][:, j, columns], in0=product[:, columns],
+                            scalar1=w_scalar[:, j : j + 1], scalar2=bias_mix[:, j, head : head + 1],
+                            op0=MULT, op1=ADD,
+                        )
 
         def add_stream_1(r):
             for j in range(NS):
@@ -242,44 +246,53 @@ def tile_crossmultiheadattention_pa_kernel(
 
         def turn_back(r):
             for j in range(NS):
-                turned_back[j, r] = turn_psum.tile([P, TILES, DH], F32, name="back", tag="turn")
+                turned_back[j, r] = turn_psum.tile([P, SEQ], F32, name="back", tag="turn")
                 parts = [mixes[r][:, j, :]]
                 if j in scalar_outputs(r):
                     parts.append(terms[j, r][:])
-                for m in range(TILES):
+                for b in range(SEQ // P):
                     for n, part in enumerate(parts):
                         nc.tensor.matmul(
-                            turned_back[j, r][:, m, :], lhsT=part[:, m * P : (m + 1) * P],
-                            rhs=ident[:], is_transpose=True,
+                            turned_back[j, r][:, b * P : (b + 1) * P],
+                            lhsT=part[:, b * P : (b + 1) * P], rhs=ident[:], is_transpose=True,
                             start=(n == 0), stop=(n == len(parts) - 1),
                         )
 
         def copy_stream_2(r):
             copied[r] = copied_pool.tile([P, SEQ], F32, name="copied")
-            nc.scalar.copy(out=copied[r][:], in_=banks[2, r][:].rearrange("p m c -> p (m c)"))
+            nc.scalar.copy(out=copied[r][:], in_=banks[2, r][:])
 
         def finish(r):
-            batch, head = ORDER[r]
-            half = r % 2
-            if half == 0:
-                results[r] = out_pool.tile([P, NS, 2, SEQ], F32, name="result")
+            batch, heads, halves = ORDER[r]
+            odd = r % 2
+            if not odd:
+                results[r] = out_pool.tile([P, NS, 2, 2 * TILES, DH], F32, name="result")
                 results[r + 1] = results[r]
             for j in range(NS):
+                if len(heads) == 1:
+                    out = results[r][:, j, odd, :, :]
+                else:
+                    out = results[r][:, j, :, odd * TILES : (odd + 1) * TILES, :]
+                out = out.rearrange("p m c -> p (m c)") if len(heads) == 1 else out.rearrange("p h m c -> p h (m c)")
+                in0 = copied[r][:]
+                in1 = turned_back[j, r][:]
+                if len(heads) == 2:
+                    in0 = in0.rearrange("p (h t) -> p h t", h=2)
+                    in1 = in1.rearrange("p (h t) -> p h t", h=2)
                 nc.vector.scalar_tensor_tensor(
-                    out=results[r][:, j, half, :], in0=copied[r][:],
-                    scalar=w_scalar[:, 2 * NS + j : 2 * NS + j + 1],
-                    in1=turned_back[j, r][:].rearrange("p m c -> p (m c)"),
+                    out=out, in0=in0, scalar=w_scalar[:, 2 * NS + j : 2 * NS + j + 1], in1=in1,
                     op0=MULT, op1=ADD,
                 )
                 if r >= ROUNDS - 2:
                     nc.sync.dma_start(
-                        out=outs[j][batch, head].rearrange("(p m) c -> p (m c)", m=TILES),
-                        in_=results[r][:, j, half, :],
+                        out=outs[j][batch, heads[0]].rearrange("(p m) c -> p (m c)", p=P),
+                        in_=results[r][:, j, odd, :, :].rearrange("p m c -> p (m c)"),
                     )
-                elif half == 1:
+                elif odd:
+                    first = heads[0] // 2 * 2
                     nc.sync.dma_start(
-                        out=outs[j][batch, head - 1 : head + 1].rearrange("h (p m) c -> p h (m c)", m=TILES),
-                        in_=results[r][:, j, :, :],
+                        out=outs[j][batch, first : first + 2].rearrange("h (p m) c -> p h (m c)", p=P),
+                        in_=results[r][:, j, :, :, :].rearrange("p h m c -> p h (m c)"),
                     )
 
         ident = keep.tile([P, P], F32)
@@ -298,95 +311,126 @@ def tile_crossmultiheadattention_pa_kernel(
             )
 
         for i in range(NS):
-            load_x(i, 0)
+            load_x(i, 0, 0)
             load_w(i, 0, 1)
+        for i in range(NS):
+            load_x(i, 0, 1)
 
         nc.vector.tensor_copy(out=w_scalar[:], in_=w_bf16[:])
         ctx.enter_context(tc.manual_schedule())
 
-        turn_head(0)
-        load_w(0, 1, 2)
-        load_x(0, 1)
-        load_w(1, 1, 2)
+        def mix_biases():
+            bias_f32 = keep.tile([P, P], F32, name="bias_f32")
+            nc.vector.tensor_copy(out=bias_f32[:], in_=bias_rows[:])
+            bias_cols = turn_psum.tile([P, SEQ], F32, name="bias_cols", tag="turn")
+            nc.tensor.transpose(bias_cols[:, 0:P], bias_f32[:], ident[:])
+            for j in range(NS):
+                nc.vector.tensor_scalar_mul(
+                    out=bias_mix[:, j, :], in0=bias_cols[:, 0:HEADS], scalar1=w_scalar[:, j : j + 1]
+                )
+            for i in range(1, NS):
+                for j in range(NS):
+                    nc.vector.scalar_tensor_tensor(
+                        out=bias_mix[:, j, :], in0=bias_cols[:, i * HEADS : (i + 1) * HEADS],
+                        scalar=w_scalar[:, NS * i + j : NS * i + j + 1], in1=bias_mix[:, j, :],
+                        op0=MULT, op1=ADD,
+                    )
+
+        bias_mix = keep.tile([P, NS, HEADS], F32)
+
+        turn_x(0, 0, 0)
+        for i in range(NS):
+            load_w(i, 1, 2)
         group_w(0, 0)
-        quantise_x(0, 0)
+        quantise_x(0, 0, 0)
+        turn_x(1, 0, 0)
         quantise_w(0, 0)
-        load_x(1, 1)
-        load_w(2, 1, 2)
-        turn_head(1)
-        load_x(2, 1)
+        mix_biases()
         project_features(0, 0)
         group_w(1, 0)
-        bias_f32 = keep.tile([P, P], F32)
-        nc.vector.tensor_copy(out=bias_f32[:], in_=bias_rows[:])
-        bias_cols = turn_psum.tile([P, P], F32, tag="turn")
-        nc.tensor.transpose(bias_cols[:], bias_f32[:], ident[:])
-        bias_mix = keep.tile([P, NS, HEADS], F32)
-        for j in range(NS):
-            nc.vector.tensor_scalar_mul(
-                out=bias_mix[:, j, :], in0=bias_cols[:, 0:HEADS], scalar1=w_scalar[:, j : j + 1]
-            )
-        for i in range(1, NS):
-            for j in range(NS):
-                nc.vector.scalar_tensor_tensor(
-                    out=bias_mix[:, j, :], in0=bias_cols[:, i * HEADS : (i + 1) * HEADS],
-                    scalar=w_scalar[:, NS * i + j : NS * i + j + 1], in1=bias_mix[:, j, :],
-                    op0=MULT, op1=ADD,
-                )
-        quantise_x(1, 0)
-        quantise_w(1, 0)
+        quantise_x(1, 0, 0)
         begin_mix(0)
-        turn_head(2)
+        turn_x(2, 0, 0)
+        quantise_w(1, 0)
         project_features(1, 0)
-        project_features(0, 1)
         make_terms(0)
         group_w(2, 0)
+        turn_x(0, 0, 1)
+        quantise_x(2, 0, 0)
         add_stream_1(0)
-        quantise_x(2, 0)
-        begin_mix(1)
+        turn_x(1, 0, 1)
+        turn_x(2, 0, 1)
+        for i in range(NS):
+            load_w(i, 2, 4)
+        for i, half in ((0, 0), (1, 0), (0, 1), (1, 1), (2, 0), (2, 1)):
+            load_x(i, 1, half)
         quantise_w(2, 0)
         project_tokens(2, 0)
+        turn_back(0)
+        copy_stream_2(0)
+        quantise_x(0, 0, 1)
+        project_features(0, 1)
+        group_w(0, 1)
+        begin_mix(1)
+        quantise_x(1, 0, 1)
         project_features(1, 1)
         make_terms(1)
-        group_w(0, 1)
-        copy_stream_2(0)
-        group_w(1, 1)
+        finish(0)
+        quantise_x(2, 0, 1)
+        project_tokens(2, 1)
+        copy_stream_2(1)
         quantise_w(0, 1)
-        turn_later(0)
         project_features(0, 2)
+        group_w(1, 1)
+        add_stream_1(1)
+        turn_back(1)
         begin_mix(2)
-        quantise_w(1, 1)
         group_w(2, 1)
-        turn_later(1)
+        group_w(0, 2)
+        quantise_w(1, 1)
+        project_features(1, 2)
+        make_terms(2)
+        finish(1)
+        quantise_w(2, 1)
+        project_tokens(2, 2)
+        copy_stream_2(2)
+        project_features(0, 3)
+        begin_mix(3)
+        group_w(1, 2)
+        add_stream_1(2)
+        project_features(1, 3)
+        make_terms(3)
+        quantise_w(0, 2)
+        project_features(0, 4)
+        begin_mix(4)
+        group_w(2, 2)
 
-        for r in range(ROUNDS):
-            if r == 1:
-                for i in range(NS):
-                    load_w(i, 2, 4)
+        for r in range(2, ROUNDS):
             turn_back(r)
-            if 0 <= r < 2:
-                turn_later(2 * r + 2)
+            for i, half in TURN_BEFORE.get(r, []):
+                turn_x(i, 1, half)
             if r + 1 < ROUNDS:
                 add_stream_1(r + 1)
+            for i, half in QX_EARLY.get(r, []):
+                quantise_x(i, 1, half)
+            for i, q in QW_EARLY.get(r, []):
+                quantise_w(i, q)
             if r + 1 < ROUNDS:
                 project_tokens(2, r + 1)
             if r + 2 < ROUNDS:
                 project_features(1, r + 2)
                 make_terms(r + 2)
-            if r + 3 < ROUNDS:
-                project_features(0, r + 3)
-                begin_mix(r + 3)
             if r + 1 < ROUNDS:
                 copy_stream_2(r + 1)
             finish(r)
-            for (i, q), when in W_ROUND.items():
-                if when == r:
-                    quantise_w(i, q)
-            for i, when in X_ROUND.items():
-                if when == r:
-                    quantise_x(i, 1)
-            for (i, q), when in W_ROUND.items():
-                if when == r + 1:
-                    group_w(i, q)
-            if 0 <= r < 2:
-                turn_later(2 * r + 3)
+            for i, q in QUANTISE_W.get(r, []):
+                quantise_w(i, q)
+            for i, half in QUANTISE_X.get(r, []):
+                quantise_x(i, 1, half)
+            if r + 3 < ROUNDS:
+                project_features(0, r + 3)
+                begin_mix(r + 3)
+            for i, q in REGROUP_W.get(r, []):
+                group_w(i, q)
+            for i, half in TURN_AFTER.get(r, []):
+                turn_x(i, 1, half)

@@ -35,7 +35,9 @@ def halved(b, h):
 ORDER = halved(0, 0) + whole(0, 2) + whole(0, 4) + halved(1, 0) + whole(1, 2) + whole(1, 4) + whole(0, 6) + whole(1, 6)
 ROUNDS = len(ORDER)
 SCALAR_BEGINS = 3
-HEAD_VECTOR = [(0, 0, 1), (1, 0, 1), (2, 0, 1)]
+SCALAR_BEGINS_LATE = 13
+GPSIMD_ADDS = 11
+HEAD_VECTOR = [(0, 0, 1)]
 QUANTISE_W = {2: [(2, 2)], 8: [(0, 3)], 9: [(1, 3)], 10: [(2, 3)]}
 QW_EARLY = {2: [(1, 2)]}
 QUANTISE_X = {2: [(0, 0)], 3: [(1, 0), (0, 1)], 4: [(1, 1), (2, 0)], 5: [(2, 1)]}
@@ -68,7 +70,7 @@ def tile_crossmultiheadattention_pa_kernel(
         w_raw_pool = ctx.enter_context(tc.tile_pool(name="w_raw", bufs=NS))
         x_grouped_pool = ctx.enter_context(tc.tile_pool(name="x_grouped", bufs=4))
         w_grouped_pool = ctx.enter_context(tc.tile_pool(name="w_grouped", bufs=3))
-        mix_pool = ctx.enter_context(tc.tile_pool(name="mix", bufs=5))
+        mix_pool = ctx.enter_context(tc.tile_pool(name="mix", bufs=4))
         term_pool = ctx.enter_context(tc.tile_pool(name="term", bufs=3))
         copied_pool = ctx.enter_context(tc.tile_pool(name="copied", bufs=3))
         out_pool = ctx.enter_context(tc.tile_pool(name="out", bufs=2))
@@ -209,13 +211,13 @@ def tile_crossmultiheadattention_pa_kernel(
             heads = ORDER[r][1]
             width = SEQ // len(heads)
             mixes[r] = mix_pool.tile([P, NS, SEQ], F32, name="mix")
-            if r >= SCALAR_BEGINS:
+            if SCALAR_BEGINS <= r < SCALAR_BEGINS_LATE:
                 product = copied_pool.tile([P, SEQ], F32, name="product")
                 nc.scalar.copy(out=product[:], in_=banks[0, r][:])
             for j in range(NS):
                 for n, head in enumerate(heads):
                     columns = slice(n * width, (n + 1) * width)
-                    if r < SCALAR_BEGINS:
+                    if r < SCALAR_BEGINS or r >= SCALAR_BEGINS_LATE:
                         nc.scalar.activation(
                             out=mixes[r][:, j, columns], in_=banks[0, r][:, columns], func=IDENTITY,
                             scale=w_scalar[:, j : j + 1], bias=bias_mix[:, j, head : head + 1],
@@ -236,6 +238,13 @@ def tile_crossmultiheadattention_pa_kernel(
                         op0=MULT, op1=ADD,
                     )
 
+        def add_terms(r):
+            if r >= GPSIMD_ADDS:
+                for j in scalar_outputs(r):
+                    nc.gpsimd.tensor_tensor(
+                        out=mixes[r][:, j, :], in0=mixes[r][:, j, :], in1=terms[j, r][:], op=ADD
+                    )
+
         def make_terms(r):
             for j in scalar_outputs(r):
                 terms[j, r] = term_pool.tile([P, SEQ], F32, name="term")
@@ -248,7 +257,7 @@ def tile_crossmultiheadattention_pa_kernel(
             for j in range(NS):
                 turned_back[j, r] = turn_psum.tile([P, SEQ], F32, name="back", tag="turn")
                 parts = [mixes[r][:, j, :]]
-                if j in scalar_outputs(r):
+                if j in scalar_outputs(r) and r < GPSIMD_ADDS:
                     parts.append(terms[j, r][:])
                 for b in range(SEQ // P):
                     for n, part in enumerate(parts):
@@ -295,22 +304,24 @@ def tile_crossmultiheadattention_pa_kernel(
                         in_=results[r][:, j, :, :, :].rearrange("p h m c -> p h (m c)"),
                     )
 
+        load_x(0, 0, 0)
         ident = keep.tile([P, P], F32)
         masks.make_identity(nc, ident[:])
         w_bf16 = keep.tile([P, NS * NS], BF16)
         w_scalar = keep.tile([P, NS * NS], F32)
-        nc.scalar.dma_start(
+        nc.sync.dma_start(
             out=w_bf16[:], in_=w_matrix.rearrange("i j -> (i j)").partition_broadcast(P)
         )
         bias_rows = keep.tile([P, P], BF16)
         nc.vector.memset(bias_rows[:], 0.0)
         for i in range(NS):
-            nc.scalar.dma_start(
+            nc.sync.dma_start(
                 out=bias_rows[i * HEADS : (i + 1) * HEADS, :],
                 in_=biases[i].rearrange("(h c) -> h c", c=DH),
             )
 
-        for i in range(NS):
+        load_w(0, 0, 1)
+        for i in range(1, NS):
             load_x(i, 0, 0)
             load_w(i, 0, 1)
         for i in range(NS):
@@ -338,6 +349,7 @@ def tile_crossmultiheadattention_pa_kernel(
 
         bias_mix = keep.tile([P, NS, HEADS], F32)
 
+        mix_biases()
         turn_x(0, 0, 0)
         for i in range(NS):
             load_w(i, 1, 2)
@@ -345,7 +357,6 @@ def tile_crossmultiheadattention_pa_kernel(
         quantise_x(0, 0, 0)
         turn_x(1, 0, 0)
         quantise_w(0, 0)
-        mix_biases()
         project_features(0, 0)
         group_w(1, 0)
         quantise_x(1, 0, 0)
@@ -415,11 +426,13 @@ def tile_crossmultiheadattention_pa_kernel(
                 quantise_x(i, 1, half)
             for i, q in QW_EARLY.get(r, []):
                 quantise_w(i, q)
-            if r + 1 < ROUNDS:
-                project_tokens(2, r + 1)
             if r + 2 < ROUNDS:
                 project_features(1, r + 2)
                 make_terms(r + 2)
+            if r + 1 < ROUNDS:
+                project_tokens(2, r + 1)
+            if r + 2 < ROUNDS:
+                add_terms(r + 2)
             if r + 1 < ROUNDS:
                 copy_stream_2(r + 1)
             finish(r)

@@ -309,13 +309,13 @@ def tile_crossmultiheadattention_pa_kernel(
         masks.make_identity(nc, ident[:])
         w_bf16 = keep.tile([P, NS * NS], BF16)
         w_scalar = keep.tile([P, NS * NS], F32)
-        nc.sync.dma_start(
+        nc.scalar.dma_start(
             out=w_bf16[:], in_=w_matrix.rearrange("i j -> (i j)").partition_broadcast(P)
         )
         bias_rows = keep.tile([P, P], BF16)
         nc.vector.memset(bias_rows[:], 0.0)
         for i in range(NS):
-            nc.sync.dma_start(
+            nc.scalar.dma_start(
                 out=bias_rows[i * HEADS : (i + 1) * HEADS, :],
                 in_=biases[i].rearrange("(h c) -> h c", c=DH),
             )
@@ -349,7 +349,6 @@ def tile_crossmultiheadattention_pa_kernel(
 
         bias_mix = keep.tile([P, NS, HEADS], F32)
 
-        mix_biases()
         turn_x(0, 0, 0)
         for i in range(NS):
             load_w(i, 1, 2)
@@ -357,6 +356,7 @@ def tile_crossmultiheadattention_pa_kernel(
         quantise_x(0, 0, 0)
         turn_x(1, 0, 0)
         quantise_w(0, 0)
+        mix_biases()
         project_features(0, 0)
         group_w(1, 0)
         quantise_x(1, 0, 0)

@@ -36,7 +36,7 @@ ORDER = halved(0, 0) + whole(0, 2) + whole(0, 4) + halved(1, 0) + whole(1, 2) + 
 ROUNDS = len(ORDER)
 SCALAR_BEGINS = 3
 SCALAR_BEGINS_LATE = 13
-GPSIMD_ADDS = 11
+GPSIMD_ADDS = 16
 HEAD_VECTOR = [(0, 0, 1)]
 QUANTISE_W = {2: [(2, 2)], 8: [(0, 3)], 9: [(1, 3)], 10: [(2, 3)]}
 QW_EARLY = {2: [(1, 2)]}

@@ -34,8 +34,7 @@ def halved(b, h):
 
 ORDER = halved(0, 0) + whole(0, 2) + whole(0, 4) + halved(1, 0) + whole(1, 2) + whole(1, 4) + whole(0, 6) + whole(1, 6)
 ROUNDS = len(ORDER)
-SCALAR_BEGINS = 3
-SCALAR_BEGINS_LATE = 13
+SCALAR_BEGINS = (0, 1, 2, 13, 14, 15)
 GPSIMD_ADDS = 16
 HEAD_VECTOR = [(0, 0, 1)]
 QUANTISE_W = {2: [(2, 2)], 8: [(0, 3)], 9: [(1, 3)], 10: [(2, 3)]}
@@ -66,14 +65,14 @@ def tile_crossmultiheadattention_pa_kernel(
 
     with ExitStack() as ctx:
         keep = ctx.enter_context(tc.tile_pool(name="keep", bufs=1))
-        x_raw_pool = ctx.enter_context(tc.tile_pool(name="x_raw", bufs=7))
+        x_raw_pool = ctx.enter_context(tc.tile_pool(name="x_raw", bufs=6))
         w_raw_pool = ctx.enter_context(tc.tile_pool(name="w_raw", bufs=NS))
-        x_grouped_pool = ctx.enter_context(tc.tile_pool(name="x_grouped", bufs=4))
+        x_grouped_pool = ctx.enter_context(tc.tile_pool(name="x_grouped", bufs=3))
         w_grouped_pool = ctx.enter_context(tc.tile_pool(name="w_grouped", bufs=3))
         mix_pool = ctx.enter_context(tc.tile_pool(name="mix", bufs=4))
         term_pool = ctx.enter_context(tc.tile_pool(name="term", bufs=3))
         copied_pool = ctx.enter_context(tc.tile_pool(name="copied", bufs=3))
-        out_pool = ctx.enter_context(tc.tile_pool(name="out", bufs=2))
+        out_pool = ctx.enter_context(tc.tile_pool(name="out", bufs=3))
         product_psum = ctx.enter_context(tc.psum_pool(name="product_psum", bufs=1))
         turn_psum = ctx.enter_context(tc.psum_pool(name="turn_psum", bufs=5))
 
@@ -211,13 +210,13 @@ def tile_crossmultiheadattention_pa_kernel(
             heads = ORDER[r][1]
             width = SEQ // len(heads)
             mixes[r] = mix_pool.tile([P, NS, SEQ], F32, name="mix")
-            if SCALAR_BEGINS <= r < SCALAR_BEGINS_LATE:
+            if r not in SCALAR_BEGINS:
                 product = copied_pool.tile([P, SEQ], F32, name="product")
                 nc.scalar.copy(out=product[:], in_=banks[0, r][:])
             for j in range(NS):
                 for n, head in enumerate(heads):
                     columns = slice(n * width, (n + 1) * width)
-                    if r < SCALAR_BEGINS or r >= SCALAR_BEGINS_LATE:
+                    if r in SCALAR_BEGINS:
                         nc.scalar.activation(
                             out=mixes[r][:, j, columns], in_=banks[0, r][:, columns], func=IDENTITY,
                             scale=w_scalar[:, j : j + 1], bias=bias_mix[:, j, head : head + 1],
@@ -292,7 +291,7 @@ def tile_crossmultiheadattention_pa_kernel(
                     out=out, in0=in0, scalar=w_scalar[:, 2 * NS + j : 2 * NS + j + 1], in1=in1,
                     op0=MULT, op1=ADD,
                 )
-                if r >= ROUNDS - 2:
+                if len(heads) == 1:
                     nc.sync.dma_start(
                         out=outs[j][batch, heads[0]].rearrange("(p m) c -> p (m c)", p=P),
                         in_=results[r][:, j, odd, :, :].rearrange("p m c -> p (m c)"),
@@ -396,7 +395,9 @@ def tile_crossmultiheadattention_pa_kernel(
         add_stream_1(1)
         turn_back(1)
         begin_mix(2)
+        project_features(0, 3)
         group_w(2, 1)
+        begin_mix(3)
         group_w(0, 2)
         quantise_w(1, 1)
         project_features(1, 2)
@@ -405,8 +406,6 @@ def tile_crossmultiheadattention_pa_kernel(
         quantise_w(2, 1)
         project_tokens(2, 2)
         copy_stream_2(2)
-        project_features(0, 3)
-        begin_mix(3)
         group_w(1, 2)
         add_stream_1(2)
         project_features(1, 3)

@@ -34,16 +34,17 @@ def halved(b, h):
 
 ORDER = halved(0, 0) + whole(0, 2) + whole(0, 4) + halved(1, 0) + whole(1, 2) + whole(1, 4) + whole(0, 6) + whole(1, 6)
 ROUNDS = len(ORDER)
+SECOND_BANK = (7, 9, 11, 13, 15)
 SCALAR_BEGINS = (0, 1, 2, 13, 14, 15)
 GPSIMD_ADDS = 16
 HEAD_VECTOR = [(0, 0, 1)]
-QUANTISE_W = {2: [(2, 2)], 8: [(0, 3)], 9: [(1, 3)], 10: [(2, 3)]}
+QUANTISE_W = {2: [(2, 2)], 7: [(0, 3)], 8: [(1, 3)], 9: [(2, 3)]}
 QW_EARLY = {2: [(1, 2)]}
 QUANTISE_X = {2: [(0, 0)], 3: [(1, 0), (0, 1)], 4: [(1, 1), (2, 0)], 5: [(2, 1)]}
 QX_EARLY = {}
 TURN_BEFORE = {2: [(0, 0)], 3: [(0, 1)], 4: [(2, 0)]}
 TURN_AFTER = {2: [(1, 0)], 3: [(1, 1)], 4: [(2, 1)]}
-REGROUP_W = {7: [(0, 3)], 8: [(1, 3)], 9: [(2, 3)]}
+REGROUP_W = {6: [(0, 3)], 7: [(1, 3)], 8: [(2, 3)]}
 REGROUP = {1: "VS", 2: "SS", 3: "SS"}
 
 FLOPS = 2 * NS * BATCH * SEQ * D * D
@@ -175,7 +176,10 @@ def tile_crossmultiheadattention_pa_kernel(
 
         def project_features(i, r):
             batch, heads, halves = ORDER[r]
-            bank = product_psum.tile([P, SEQ], F32, name="p_%d" % i, tag="p_%d" % i)
+            if i == 1 and r in SECOND_BANK:
+                bank = turn_psum.tile([P, SEQ], F32, name="p_turn", tag="turn")
+            else:
+                bank = product_psum.tile([P, SEQ], F32, name="p_%d" % i, tag="p_%d" % i)
             banks[i, r] = bank
             for n, (head, half) in enumerate([(head, half) for head in heads for half in halves]):
                 for g in range(PASSES):

@@ -38,20 +38,20 @@ SECOND_BANK = (7, 9, 11, 13, 15)
 SCALAR_BEGINS = (0, 1, 2, 13, 14, 15)
 GPSIMD_ADDS = 16
 HEAD_VECTOR = [(0, 0, 1)]
-QUANTISE_W = {2: [(2, 2)], 7: [(0, 3)], 8: [(1, 3)], 9: [(2, 3)]}
+QUANTISE_W = {2: [(2, 2)], 8: [(0, 3), (1, 3)], 9: [(2, 3)]}
 QW_EARLY = {2: [(1, 2)]}
 QUANTISE_X = {2: [(0, 0)], 3: [(1, 0), (0, 1)], 4: [(1, 1), (2, 0)], 5: [(2, 1)]}
 QX_EARLY = {}
 TURN_BEFORE = {2: [(0, 0)], 3: [(0, 1)], 4: [(2, 0)]}
 TURN_AFTER = {2: [(1, 0)], 3: [(1, 1)], 4: [(2, 1)]}
-REGROUP_W = {6: [(0, 3)], 7: [(1, 3)], 8: [(2, 3)]}
+REGROUP_W = {7: [(1, 3)], 8: [(2, 3)]}
 REGROUP = {1: "VS", 2: "SS", 3: "SS"}
 
 FLOPS = 2 * NS * BATCH * SEQ * D * D
 
 
 def scalar_outputs(r):
-    return range(NS - (1 if r >= 6 else 0), NS)
+    return range(NS - (1 if r >= 7 else 0), NS)
 
 
 def tile_crossmultiheadattention_pa_kernel(
@@ -323,10 +323,11 @@ def tile_crossmultiheadattention_pa_kernel(
                 in_=biases[i].rearrange("(h c) -> h c", c=DH),
             )
 
+        load_x(1, 0, 0)
         load_w(0, 0, 1)
-        for i in range(1, NS):
-            load_x(i, 0, 0)
-            load_w(i, 0, 1)
+        load_w(1, 0, 1)
+        load_x(2, 0, 0)
+        load_w(2, 0, 1)
         for i in range(NS):
             load_x(i, 0, 1)
 
@@ -355,8 +356,8 @@ def tile_crossmultiheadattention_pa_kernel(
         turn_x(0, 0, 0)
         for i in range(NS):
             load_w(i, 1, 2)
-        group_w(0, 0)
         quantise_x(0, 0, 0)
+        group_w(0, 0)
         turn_x(1, 0, 0)
         quantise_w(0, 0)
         mix_biases()
@@ -387,11 +388,11 @@ def tile_crossmultiheadattention_pa_kernel(
         group_w(0, 1)
         begin_mix(1)
         quantise_x(1, 0, 1)
+        quantise_x(2, 0, 1)
+        project_tokens(2, 1)
         project_features(1, 1)
         make_terms(1)
         finish(0)
-        quantise_x(2, 0, 1)
-        project_tokens(2, 1)
         copy_stream_2(1)
         quantise_w(0, 1)
         project_features(0, 2)
@@ -421,6 +422,8 @@ def tile_crossmultiheadattention_pa_kernel(
 
         for r in range(2, ROUNDS):
             turn_back(r)
+            if r == 6:
+                group_w(0, 3)
             for i, half in TURN_BEFORE.get(r, []):
                 turn_x(i, 1, half)
             if r + 1 < ROUNDS:

@@ -37,6 +37,7 @@ ROUNDS = len(ORDER)
 SECOND_BANK = (7, 9, 11, 13, 15)
 SCALAR_BEGINS = (0, 1, 2, 13, 14, 15)
 GPSIMD_ADDS = 16
+WARM_BACK = (1, 3)
 HEAD_VECTOR = [(0, 0, 1)]
 QUANTISE_W = {2: [(2, 2)], 8: [(0, 3), (1, 3)], 9: [(2, 3)]}
 QW_EARLY = {2: [(1, 2)]}
@@ -147,6 +148,9 @@ def tile_crossmultiheadattention_pa_kernel(
         def x_columns(g, first, count):
             return slice(g * HALF + first * P, g * HALF + (first + count) * P)
 
+        def warm(bank):
+            nc.tensor.matmul(bank, lhsT=zeros[:, 0:P], rhs=zeros[:], start=True, stop=True)
+
         def turn_x(i, batch, half):
             x_grouped[i, batch, half] = x_grouped_pool.tile(
                 [P, PASSES, TILES, P * PACK], BF16, name="x_grouped", align_bytes=64
@@ -156,6 +160,8 @@ def tile_crossmultiheadattention_pa_kernel(
                     "r (g u p) -> r g u p", g=PASSES, u=2
                 )
                 turned = turn_psum.tile([P, PASSES * 2, P], F32, name="turned", tag="turn")
+                if batch == 0 and m == 0:
+                    warm(turned[:].rearrange("p u r -> p (u r)"))
                 for g in range(PASSES):
                     for u in range(2):
                         nc.tensor.transpose(turned[:, 2 * g + u, :], words[:, g, u, :], ident[:])
@@ -259,6 +265,8 @@ def tile_crossmultiheadattention_pa_kernel(
         def turn_back(r):
             for j in range(NS):
                 turned_back[j, r] = turn_psum.tile([P, SEQ], F32, name="back", tag="turn")
+                if r in WARM_BACK:
+                    warm(turned_back[j, r][:])
                 parts = [mixes[r][:, j, :]]
                 if j in scalar_outputs(r) and r < GPSIMD_ADDS:
                     parts.append(terms[j, r][:])
@@ -308,6 +316,8 @@ def tile_crossmultiheadattention_pa_kernel(
                     )
 
         load_x(0, 0, 0)
+        zeros = keep.tile([P, SEQ], BF16)
+        nc.vector.memset(zeros[:], 0.0)
         ident = keep.tile([P, P], F32)
         masks.make_identity(nc, ident[:])
         w_bf16 = keep.tile([P, NS * NS], BF16)

@@ -37,7 +37,7 @@ ROUNDS = len(ORDER)
 SECOND_BANK = (7, 9, 11, 13, 15)
 SCALAR_BEGINS = (0, 1, 2, 13, 14, 15)
 GPSIMD_ADDS = 16
-WARM_BACK = (1, 3)
+PLAIN_BACK = (1, 2, 3, 4)
 HEAD_VECTOR = [(0, 0, 1)]
 QUANTISE_W = {2: [(2, 2)], 8: [(0, 3), (1, 3)], 9: [(2, 3)]}
 QW_EARLY = {2: [(1, 2)]}
@@ -265,8 +265,6 @@ def tile_crossmultiheadattention_pa_kernel(
         def turn_back(r):
             for j in range(NS):
                 turned_back[j, r] = turn_psum.tile([P, SEQ], F32, name="back", tag="turn")
-                if r in WARM_BACK:
-                    warm(turned_back[j, r][:])
                 parts = [mixes[r][:, j, :]]
                 if j in scalar_outputs(r) and r < GPSIMD_ADDS:
                     parts.append(terms[j, r][:])
@@ -274,7 +272,8 @@ def tile_crossmultiheadattention_pa_kernel(
                     for n, part in enumerate(parts):
                         nc.tensor.matmul(
                             turned_back[j, r][:, b * P : (b + 1) * P],
-                            lhsT=part[:, b * P : (b + 1) * P], rhs=ident[:], is_transpose=True,
+                            lhsT=part[:, b * P : (b + 1) * P], rhs=ident[:],
+                            is_transpose=not (b == 2 and r in PLAIN_BACK),
                             start=(n == 0), stop=(n == len(parts) - 1),
                         )
 

@@ -36,7 +36,7 @@ ORDER = halved(0, 0) + whole(0, 2) + whole(0, 4) + halved(1, 0) + whole(1, 2) + 
 ROUNDS = len(ORDER)
 SECOND_BANK = (7, 9, 11, 13, 15)
 SCALAR_BEGINS = (0, 1, 2, 13, 14, 15)
-GPSIMD_ADDS = 16
+GPSIMD_ADDS = 13
 PLAIN_BACK = (1, 2, 3, 4)
 HEAD_VECTOR = [(0, 0, 1)]
 QUANTISE_W = {2: [(2, 2)], 8: [(0, 3), (1, 3)], 9: [(2, 3)]}

from contextlib import ExitStack

import concourse.masks as masks
import concourse.mybir as mybir

F32 = mybir.dt.float32
BF16 = mybir.dt.bfloat16
U32 = mybir.dt.uint32
U8 = mybir.dt.uint8
FP8X4 = mybir.dt.float8_e4m3fn_x4
MULT = mybir.AluOpType.mult
ADD = mybir.AluOpType.add
IDENTITY = mybir.ActivationFunctionType.Identity

P = 128
PACK = 4
BATCH, SEQ, D, HEADS, NS = 2, 512, 1024, 8, 3
DH = D // HEADS
PASSES = D // (P * PACK)
HALVES = 2
TILES = SEQ // P // HALVES
HALF = SEQ // HALVES
PIECE = 2 * DH
QUARTERS = D // PIECE
RUN = 4
VECTOR_COLUMNS = 160
def whole(b, h):
    return [(b, [h], [0, 1]), (b, [h + 1], [0, 1])]


def halved(b, h):
    return [(b, [h, h + 1], [0]), (b, [h, h + 1], [1])]


ORDER = halved(0, 0) + whole(0, 2) + whole(0, 4) + halved(1, 0) + whole(1, 2) + whole(1, 4) + whole(0, 6) + whole(1, 6)
ROUNDS = len(ORDER)
SECOND_BANK = (7, 9, 11, 13, 15)
SCALAR_BEGINS = (0, 1, 2, 13, 14, 15)
GPSIMD_ADDS = 13
PLAIN_BACK = (1, 2, 3, 4)
HEAD_VECTOR = [(0, 0, 1)]
QUANTISE_W = {2: [(2, 2)], 8: [(0, 3), (1, 3)], 9: [(2, 3)]}
QW_EARLY = {2: [(1, 2)]}
QUANTISE_X = {2: [(0, 0)], 3: [(1, 0), (0, 1)], 4: [(1, 1), (2, 0)], 5: [(2, 1)]}
QX_EARLY = {}
TURN_BEFORE = {2: [(0, 0)], 3: [(0, 1)], 4: [(2, 0)]}
TURN_AFTER = {2: [(1, 0)], 3: [(1, 1)], 4: [(2, 1)]}
REGROUP_W = {7: [(1, 3)], 8: [(2, 3)]}
REGROUP = {1: "VS", 2: "SS", 3: "SS"}

FLOPS = 2 * NS * BATCH * SEQ * D * D


def scalar_outputs(r):
    return range(NS - (1 if r >= 7 else 0), NS)


def tile_crossmultiheadattention_pa_kernel(
    tc, input_tensor, position_embedding, attr, Wq, bq, Wqp, bqp, Wqa, bqa, w_matrix,
    out_0, out_1, out_2,
):
    nc = tc.nc
    streams = [input_tensor, position_embedding, attr]
    weights = [Wq, Wqp, Wqa]
    biases = [bq, bqp, bqa]
    outs = [out_0, out_1, out_2]

    with ExitStack() as ctx:
        keep = ctx.enter_context(tc.tile_pool(name="keep", bufs=1))
        x_raw_pool = ctx.enter_context(tc.tile_pool(name="x_raw", bufs=6))
        w_raw_pool = ctx.enter_context(tc.tile_pool(name="w_raw", bufs=NS))
        x_grouped_pool = ctx.enter_context(tc.tile_pool(name="x_grouped", bufs=3))
        w_grouped_pool = ctx.enter_context(tc.tile_pool(name="w_grouped", bufs=3))
        mix_pool = ctx.enter_context(tc.tile_pool(name="mix", bufs=4))
        term_pool = ctx.enter_context(tc.tile_pool(name="term", bufs=3))
        copied_pool = ctx.enter_context(tc.tile_pool(name="copied", bufs=3))
        out_pool = ctx.enter_context(tc.tile_pool(name="out", bufs=3))
        product_psum = ctx.enter_context(tc.psum_pool(name="product_psum", bufs=1))
        turn_psum = ctx.enter_context(tc.psum_pool(name="turn_psum", bufs=5))

        x_codes = keep.tile([P, NS, BATCH, HALVES, PASSES * HALF], U32, align_bytes=64)
        x_scales = keep.tile([P, NS, BATCH, HALVES, PASSES * HALF], U8, align_bytes=64)
        w_codes = keep.tile([P, NS, QUARTERS, PASSES * PIECE], U32, align_bytes=64)
        w_scales = keep.tile([P, NS, QUARTERS, PASSES * PIECE], U8, align_bytes=64)

        x_raw = {}
        x_grouped = {}
        w_raw = {}
        w_grouped = {}
        banks = {}
        mixes = {}
        terms = {}
        copied = {}
        results = {}
        turned_back = {}

        def load_x(i, batch, half):
            x_raw[i, batch, half] = x_raw_pool.tile([P, TILES, D], BF16, name="x_raw")
            rows = streams[i][batch].rearrange("(p m) k -> p m k", p=P)
            nc.sync.dma_start(
                out=x_raw[i, batch, half][:], in_=rows[:, half * TILES : (half + 1) * TILES, :]
            )

        def load_w(i, first, last):
            tile = w_raw_pool.tile(
                [P, PASSES, PACK, (last - first) * PIECE], BF16, name="w_raw_%d_%d" % (first, last)
            )
            rows = weights[i][:, first * PIECE : last * PIECE].rearrange(
                "(v p e) n -> v p e n", p=P, e=2
            )
            for g in range(PASSES):
                for u in range(2):
                    nc.sync.dma_start(out=tile[:, g, 2 * u : 2 * u + 2, :], in_=rows[2 * g + u])
                for q in range(first, last):
                    w_raw[i, g, q] = tile[:, g, :, (q - first) * PIECE : (q - first + 1) * PIECE]

        def regroup_w(copy, i, g, q, first, last):
            copy(
                out=w_grouped[i, q][:, g, first:last, :].rearrange("p (c r) t -> p c t r", r=RUN),
                in_=w_raw[i, g, q][:, :, first:last].rearrange("p t (c r) -> p c t r", r=RUN),
            )

        def gpsimd_copy(out, in_):
            nc.gpsimd.tensor_scalar(out=out, in0=in_, scalar1=1.0, scalar2=0.0, op0=MULT, op1=ADD)

        def group_w(i, q):
            w_grouped[i, q] = w_grouped_pool.tile(
                [P, PASSES, PIECE, PACK], BF16, name="w_grouped", align_bytes=64
            )
            for g in range(PASSES):
                if q == 0:
                    regroup_w(nc.scalar.copy, i, g, q, VECTOR_COLUMNS, PIECE)
                    regroup_w(nc.vector.tensor_copy, i, g, q, 0, VECTOR_COLUMNS)
                else:
                    regroup_w({"S": nc.scalar.copy, "G": gpsimd_copy, "V": nc.vector.tensor_copy}[REGROUP[q][g]], i, g, q, 0, PIECE)

        def quantise_w(i, q):
            nc.vector.quantize_mx(
                out=w_codes[:, i, q, :].bitcast(FP8X4),
                scales=w_scales[:, i, q, :],
                in_=w_grouped[i, q][:].rearrange("p g n t -> p (g n t)"),
            )

        def w_columns(head, g, count):
            first = g * PIECE + head % 2 * DH
            return slice(first, first + count * DH)

        def x_columns(g, first, count):
            return slice(g * HALF + first * P, g * HALF + (first + count) * P)

        def warm(bank):
            nc.tensor.matmul(bank, lhsT=zeros[:, 0:P], rhs=zeros[:], start=True, stop=True)

        def turn_x(i, batch, half):
            x_grouped[i, batch, half] = x_grouped_pool.tile(
                [P, PASSES, TILES, P * PACK], BF16, name="x_grouped", align_bytes=64
            )
            for m in range(TILES):
                words = x_raw[i, batch, half][:].bitcast(F32)[:, m, :].rearrange(
                    "r (g u p) -> r g u p", g=PASSES, u=2
                )
                turned = turn_psum.tile([P, PASSES * 2, P], F32, name="turned", tag="turn")
                if batch == 0 and m == 0:
                    warm(turned[:].rearrange("p u r -> p (u r)"))
                for g in range(PASSES):
                    for u in range(2):
                        nc.tensor.transpose(turned[:, 2 * g + u, :], words[:, g, u, :], ident[:])
                copy = nc.vector.tensor_copy if batch == 0 and (i, half, m) in HEAD_VECTOR else nc.scalar.copy
                copy(
                    out=x_grouped[i, batch, half][:].bitcast(F32)[:, :, m, :].rearrange(
                        "p g (r u) -> p g r u", u=2
                    ),
                    in_=turned[:].rearrange("p (g u) r -> p g r u", u=2),
                )

        def quantise_x(i, batch, half):
            nc.vector.quantize_mx(
                out=x_codes[:, i, batch, half, :].bitcast(FP8X4),
                scales=x_scales[:, i, batch, half, :],
                in_=x_grouped[i, batch, half][:].rearrange("p g m c -> p (g m c)"),
            )

        def project_features(i, r):
            batch, heads, halves = ORDER[r]
            if i == 1 and r in SECOND_BANK:
                bank = turn_psum.tile([P, SEQ], F32, name="p_turn", tag="turn")
            else:
                bank = product_psum.tile([P, SEQ], F32, name="p_%d" % i, tag="p_%d" % i)
            banks[i, r] = bank
            for n, (head, half) in enumerate([(head, half) for head in heads for half in halves]):
                for g in range(PASSES):
                    nc.tensor.matmul_mx(
                        out=bank[:, n * HALF : (n + 1) * HALF],
                        lhsT=w_codes[:, i, head // 2, w_columns(head, g, 1)].bitcast(FP8X4),
                        lhsT_scale=w_scales[:, i, head // 2, w_columns(head, g, 1)],
                        rhs=x_codes[:, i, batch, half, x_columns(g, 0, TILES)].bitcast(FP8X4),
                        rhs_scale=x_scales[:, i, batch, half, x_columns(g, 0, TILES)],
                        start=(g == 0),
                        stop=(g == PASSES - 1),
                    )

        def project_tokens(i, r):
            batch, heads, halves = ORDER[r]
            bank = product_psum.tile([P, SEQ], F32, name="p_%d" % i, tag="p_%d" % i)
            banks[i, r] = bank
            blocks = [(head, half, m) for head in heads for half in halves for m in range(TILES)]
            for n, (head, half, m) in enumerate(blocks):
                for g in range(PASSES):
                    nc.tensor.matmul_mx(
                        out=bank[:, n * P : (n + 1) * P],
                        lhsT=x_codes[:, i, batch, half, x_columns(g, m, 1)].bitcast(FP8X4),
                        lhsT_scale=x_scales[:, i, batch, half, x_columns(g, m, 1)],
                        rhs=w_codes[:, i, head // 2, w_columns(head, g, 1)].bitcast(FP8X4),
                        rhs_scale=w_scales[:, i, head // 2, w_columns(head, g, 1)],
                        start=(g == 0),
                        stop=(g == PASSES - 1),
                    )

        def begin_mix(r):
            heads = ORDER[r][1]
            width = SEQ // len(heads)
            mixes[r] = mix_pool.tile([P, NS, SEQ], F32, name="mix")
            if r not in SCALAR_BEGINS:
                product = copied_pool.tile([P, SEQ], F32, name="product")
                nc.scalar.copy(out=product[:], in_=banks[0, r][:])
            for j in range(NS):
                for n, head in enumerate(heads):
                    columns = slice(n * width, (n + 1) * width)
                    if r in SCALAR_BEGINS:
                        nc.scalar.activation(
                            out=mixes[r][:, j, columns], in_=banks[0, r][:, columns], func=IDENTITY,
                            scale=w_scalar[:, j : j + 1], bias=bias_mix[:, j, head : head + 1],
                        )
                    else:
                        nc.gpsimd.tensor_scalar(
                            out=mixes[r][:, j, columns], in0=product[:, columns],
                            scalar1=w_scalar[:, j : j + 1], scalar2=bias_mix[:, j, head : head + 1],
                            op0=MULT, op1=ADD,
                        )

        def add_stream_1(r):
            for j in range(NS):
                if j not in scalar_outputs(r):
                    nc.vector.scalar_tensor_tensor(
                        out=mixes[r][:, j, :], in0=banks[1, r][:],
                        scalar=w_scalar[:, NS + j : NS + j + 1], in1=mixes[r][:, j, :],
                        op0=MULT, op1=ADD,
                    )

        def add_terms(r):
            if r >= GPSIMD_ADDS:
                for j in scalar_outputs(r):
                    nc.gpsimd.tensor_tensor(
                        out=mixes[r][:, j, :], in0=mixes[r][:, j, :], in1=terms[j, r][:], op=ADD
                    )

        def make_terms(r):
            for j in scalar_outputs(r):
                terms[j, r] = term_pool.tile([P, SEQ], F32, name="term")
                nc.scalar.activation(
                    out=terms[j, r][:], in_=banks[1, r][:], func=IDENTITY,
                    scale=w_scalar[:, NS + j : NS + j + 1],
                )

        def turn_back(r):
            for j in range(NS):
                turned_back[j, r] = turn_psum.tile([P, SEQ], F32, name="back", tag="turn")
                parts = [mixes[r][:, j, :]]
                if j in scalar_outputs(r) and r < GPSIMD_ADDS:
                    parts.append(terms[j, r][:])
                for b in range(SEQ // P):
                    for n, part in enumerate(parts):
                        nc.tensor.matmul(
                            turned_back[j, r][:, b * P : (b + 1) * P],
                            lhsT=part[:, b * P : (b + 1) * P], rhs=ident[:],
                            is_transpose=not (b == 2 and r in PLAIN_BACK),
                            start=(n == 0), stop=(n == len(parts) - 1),
                        )

        def copy_stream_2(r):
            copied[r] = copied_pool.tile([P, SEQ], F32, name="copied")
            nc.scalar.copy(out=copied[r][:], in_=banks[2, r][:])

        def finish(r):
            batch, heads, halves = ORDER[r]
            odd = r % 2
            if not odd:
                results[r] = out_pool.tile([P, NS, 2, 2 * TILES, DH], F32, name="result")
                results[r + 1] = results[r]
            for j in range(NS):
                if len(heads) == 1:
                    out = results[r][:, j, odd, :, :]
                else:
                    out = results[r][:, j, :, odd * TILES : (odd + 1) * TILES, :]
                out = out.rearrange("p m c -> p (m c)") if len(heads) == 1 else out.rearrange("p h m c -> p h (m c)")
                in0 = copied[r][:]
                in1 = turned_back[j, r][:]
                if len(heads) == 2:
                    in0 = in0.rearrange("p (h t) -> p h t", h=2)
                    in1 = in1.rearrange("p (h t) -> p h t", h=2)
                nc.vector.scalar_tensor_tensor(
                    out=out, in0=in0, scalar=w_scalar[:, 2 * NS + j : 2 * NS + j + 1], in1=in1,
                    op0=MULT, op1=ADD,
                )
                if len(heads) == 1:
                    nc.sync.dma_start(
                        out=outs[j][batch, heads[0]].rearrange("(p m) c -> p (m c)", p=P),
                        in_=results[r][:, j, odd, :, :].rearrange("p m c -> p (m c)"),
                    )
                elif odd:
                    first = heads[0] // 2 * 2
                    nc.sync.dma_start(
                        out=outs[j][batch, first : first + 2].rearrange("h (p m) c -> p h (m c)", p=P),
                        in_=results[r][:, j, :, :, :].rearrange("p h m c -> p h (m c)"),
                    )

        load_x(0, 0, 0)
        zeros = keep.tile([P, SEQ], BF16)
        nc.vector.memset(zeros[:], 0.0)
        ident = keep.tile([P, P], F32)
        masks.make_identity(nc, ident[:])
        w_bf16 = keep.tile([P, NS * NS], BF16)
        w_scalar = keep.tile([P, NS * NS], F32)
        nc.scalar.dma_start(
            out=w_bf16[:], in_=w_matrix.rearrange("i j -> (i j)").partition_broadcast(P)
        )
        bias_rows = keep.tile([P, P], BF16)
        nc.vector.memset(bias_rows[:], 0.0)
        for i in range(NS):
            nc.scalar.dma_start(
                out=bias_rows[i * HEADS : (i + 1) * HEADS, :],
                in_=biases[i].rearrange("(h c) -> h c", c=DH),
            )

        load_x(1, 0, 0)
        load_w(0, 0, 1)
        load_w(1, 0, 1)
        load_x(2, 0, 0)
        load_w(2, 0, 1)
        for i in range(NS):
            load_x(i, 0, 1)

        nc.vector.tensor_copy(out=w_scalar[:], in_=w_bf16[:])
        ctx.enter_context(tc.manual_schedule())

        def mix_biases():
            bias_f32 = keep.tile([P, P], F32, name="bias_f32")
            nc.vector.tensor_copy(out=bias_f32[:], in_=bias_rows[:])
            bias_cols = turn_psum.tile([P, SEQ], F32, name="bias_cols", tag="turn")
            nc.tensor.transpose(bias_cols[:, 0:P], bias_f32[:], ident[:])
            for j in range(NS):
                nc.vector.tensor_scalar_mul(
                    out=bias_mix[:, j, :], in0=bias_cols[:, 0:HEADS], scalar1=w_scalar[:, j : j + 1]
                )
            for i in range(1, NS):
                for j in range(NS):
                    nc.vector.scalar_tensor_tensor(
                        out=bias_mix[:, j, :], in0=bias_cols[:, i * HEADS : (i + 1) * HEADS],
                        scalar=w_scalar[:, NS * i + j : NS * i + j + 1], in1=bias_mix[:, j, :],
                        op0=MULT, op1=ADD,
                    )

        bias_mix = keep.tile([P, NS, HEADS], F32)

        turn_x(0, 0, 0)
        for i in range(NS):
            load_w(i, 1, 2)
        quantise_x(0, 0, 0)
        group_w(0, 0)
        turn_x(1, 0, 0)
        quantise_w(0, 0)
        mix_biases()
        project_features(0, 0)
        group_w(1, 0)
        quantise_x(1, 0, 0)
        begin_mix(0)
        turn_x(2, 0, 0)
        quantise_w(1, 0)
        project_features(1, 0)
        make_terms(0)
        group_w(2, 0)
        turn_x(0, 0, 1)
        quantise_x(2, 0, 0)
        add_stream_1(0)
        turn_x(1, 0, 1)
        turn_x(2, 0, 1)
        for i in range(NS):
            load_w(i, 2, 4)
        for i, half in ((0, 0), (1, 0), (0, 1), (1, 1), (2, 0), (2, 1)):
            load_x(i, 1, half)
        quantise_w(2, 0)
        project_tokens(2, 0)
        turn_back(0)
        copy_stream_2(0)
        quantise_x(0, 0, 1)
        project_features(0, 1)
        group_w(0, 1)
        begin_mix(1)
        quantise_x(1, 0, 1)
        quantise_x(2, 0, 1)
        project_tokens(2, 1)
        project_features(1, 1)
        make_terms(1)
        finish(0)
        copy_stream_2(1)
        quantise_w(0, 1)
        project_features(0, 2)
        group_w(1, 1)
        add_stream_1(1)
        turn_back(1)
        begin_mix(2)
        project_features(0, 3)
        group_w(2, 1)
        begin_mix(3)
        group_w(0, 2)
        quantise_w(1, 1)
        project_features(1, 2)
        make_terms(2)
        finish(1)
        quantise_w(2, 1)
        project_tokens(2, 2)
        copy_stream_2(2)
        group_w(1, 2)
        add_stream_1(2)
        project_features(1, 3)
        make_terms(3)
        quantise_w(0, 2)
        project_features(0, 4)
        begin_mix(4)
        group_w(2, 2)

        for r in range(2, ROUNDS):
            turn_back(r)
            if r == 6:
                group_w(0, 3)
            for i, half in TURN_BEFORE.get(r, []):
                turn_x(i, 1, half)
            if r + 1 < ROUNDS:
                add_stream_1(r + 1)
            for i, half in QX_EARLY.get(r, []):
                quantise_x(i, 1, half)
            for i, q in QW_EARLY.get(r, []):
                quantise_w(i, q)
            if r + 2 < ROUNDS:
                project_features(1, r + 2)
                make_terms(r + 2)
            if r + 1 < ROUNDS:
                project_tokens(2, r + 1)
            if r + 2 < ROUNDS:
                add_terms(r + 2)
            if r + 1 < ROUNDS:
                copy_stream_2(r + 1)
            finish(r)
            for i, q in QUANTISE_W.get(r, []):
                quantise_w(i, q)
            for i, half in QUANTISE_X.get(r, []):
                quantise_x(i, 1, half)
            if r + 3 < ROUNDS:
                project_features(0, r + 3)
                begin_mix(r + 3)
            for i, q in REGROUP_W.get(r, []):
                group_w(i, q)
            for i, half in TURN_AFTER.get(r, []):
                turn_x(i, 1, half)
